import numpy as np
import ml_dtypes


def mxq(x, axis, fmt="e4m3"):
    dtype, down = {"e4m3": (ml_dtypes.float8_e4m3fn, 7), "e5m2": (ml_dtypes.float8_e5m2, 14)}[fmt]
    v = np.moveaxis(np.asarray(x, np.float32).astype(ml_dtypes.bfloat16).astype(np.float64), axis, -1)
    blocks = v.reshape(v.shape[:-1] + (-1, 32))
    amax = np.abs(blocks).max(-1, keepdims=True)
    byte = np.maximum(np.where(amax > 0, np.frexp(amax)[1] - 1 + 127, 0) - down, 1)
    scale = np.exp2(byte - 127.0)
    codes = (blocks / scale).astype(np.float32).astype(dtype).astype(np.float64)
    return np.moveaxis((codes * scale).reshape(v.shape), -1, axis)


WIDE = False


def mx_kscale(k):
    if not WIDE:
        return np.ones(k)
    levels = np.array([30, -30])
    if k % 512:
        return np.exp2(np.random.permutation(np.resize(levels, k // 32))).repeat(32)
    a = np.empty((k // 512, 16))
    for p in range(k // 512):
        a[p, :8] = np.random.permutation(np.resize(levels, 8))
        for g in range(8):
            far = levels[np.abs(levels - a[p, g]) >= 10]
            a[p, g + 8] = far[np.random.randint(len(far))]
    return np.exp2(a.ravel()).repeat(32)


BF16 = ml_dtypes.bfloat16


def bf(x):
    return np.asarray(x, np.float32).astype(BF16)


def f64(x):
    return np.asarray(x).astype(np.float64)


B, S, D, H, DK, DV, C = 1, 1024, 1024, 16, 128, 128, 512
THETA = 10000.0
SCALE_BASE = 512.0


def rotate_half(t):
    tr = t.reshape(t.shape[:-1] + (-1, 2))
    return np.stack((-tr[..., 1], tr[..., 0]), axis=-1).reshape(t.shape)


def xpos_tables():
    pos = np.arange(S, dtype=np.float64)
    even = np.arange(0, DK, 2, dtype=np.float64)
    inv_freq = 1.0 / THETA ** (even / DK)
    freqs = np.repeat(pos[:, None] * inv_freq[None, :], 2, axis=-1)
    sbase = (even + 0.4 * DK) / (1.4 * DK)
    power = (pos - S // 2) / SCALE_BASE
    scale = np.repeat(sbase[None, :] ** power[:, None], 2, axis=-1)
    return np.cos(freqs), np.sin(freqs), scale


def heads(t):
    return t.reshape(B, S, H, -1).transpose(0, 2, 1, 3)


def setup_inputs():
    s = mx_kscale(D)
    return {"x": bf(np.random.standard_normal((B, S, D)) * s),
            "Wq": bf(np.random.standard_normal((D, H * DK)) * 0.25 / np.sqrt(D) / s[:, None]),
            "bq": bf(np.random.standard_normal(H * DK) * 0.1),
            "Wk": bf(np.random.standard_normal((D, H * DK)) * 0.25 / np.sqrt(D) / s[:, None]),
            "bk": bf(np.random.standard_normal(H * DK) * 0.1)}


def reference(x, Wq, bq, Wk, bk):
    xq = mxq(f64(x), 2, "e5m2")
    q = heads((xq @ mxq(f64(Wq), 0, "e5m2")) + f64(bq))
    k = heads((xq @ mxq(f64(Wk), 0, "e5m2")) + f64(bk))
    cos, sin, scale = xpos_tables()
    q_rot = (q * cos + rotate_half(q) * sin) * scale
    k_rot = (k * cos + rotate_half(k) * sin) / scale
    return q_rot, k_rot

@@ -1,0 +1,305 @@
+from contextlib import ExitStack
+import math
+
+import concourse.mybir as mybir
+from concourse.masks import make_identity
+
+FLOPS = 2 * 1024 * 1024 * 4096
+
+F32 = mybir.dt.float32
+BF16 = mybir.dt.bfloat16
+I32 = mybir.dt.int32
+U32 = mybir.dt.uint32
+U8 = mybir.dt.uint8
+FP8X4 = mybir.dt.float8_e5m2_x4
+ALU = mybir.AluOpType
+ACT = mybir.ActivationFunctionType
+
+P = 128
+S = 1024
+D = 1024
+H = 16
+DK = 128
+TB = 8
+HALF = 512
+TWO_PI = 2.0 * math.pi
+MAGIC = 12582912.0
+NT = 2 * H
+
+
+def g_rot(i, hf):
+    return hf == 1 and i % 2 == 1
+
+
+def prep_engine(i):
+    return "v" if i < 2 else ("g" if i % 3 == 2 else "s")
+
+
+def tile_gatedmultiscaleretentionlayer_pa_kernel(tc, x, Wq, bq, Wk, bk, out_0, out_1):
+    nc = tc.nc
+    with ExitStack() as ctx:
+        keep = ctx.enter_context(tc.tile_pool(name="keep", bufs=1))
+        tmp = ctx.enter_context(tc.tile_pool(name="tmp", bufs=5))
+        grp = ctx.enter_context(tc.tile_pool(name="grp", bufs=4))
+        wcp = ctx.enter_context(tc.tile_pool(name="wcp", bufs=5))
+        uvp = ctx.enter_context(tc.tile_pool(name="uvp", bufs=4))
+        gvp = ctx.enter_context(tc.tile_pool(name="gvp", bufs=2))
+        outp = ctx.enter_context(tc.tile_pool(name="outp", bufs=6))
+        psmx = ctx.enter_context(tc.psum_pool(name="psmx", bufs=4))
+        pstp = ctx.enter_context(tc.psum_pool(name="pstp", bufs=4))
+
+        xv = x.rearrange("b (r t) k -> (b r) t k", t=TB)
+        wv = [w.rearrange("(g p j) n -> g p j n", g=2, j=4) for w in (Wq, Wk)]
+        outv = [o.rearrange("b h (r t) f -> (b h) r t f", t=TB) for o in (out_0, out_1)]
+
+        x_sb = [keep.tile([P, 2, D], BF16, name="x_sb%d" % tp) for tp in range(4)]
+        wraw = [[keep.tile([P, 2, 4, HALF], BF16, name="wraw%d_%d" % (mat, cg)) for cg in range(4)] for mat in range(2)]
+        btile = keep.tile([P, P], BF16, name="btile")
+        nc.vector.memset(btile[:], 0.0)
+
+        def load_x(tp):
+            nc.sync.dma_start(out=x_sb[tp][:], in_=xv[:, 2 * tp:2 * tp + 2, :])
+
+        def load_w(mat, cg, c0, c1):
+            for g in range(2):
+                nc.sync.dma_start(out=wraw[mat][cg][:, g, :, c0:c1], in_=wv[mat][g, :, :, cg * HALF + c0:cg * HALF + c1])
+
+        load_x(0)
+        load_x(1)
+        load_w(0, 0, 0, 256)
+        load_x(2)
+        load_x(3)
+        nc.sync.dma_start(out=btile[0:H, :], in_=bq.rearrange("(h c) -> h c", c=DK))
+        nc.sync.dma_start(out=btile[H:2 * H, :], in_=bk.rearrange("(h c) -> h c", c=DK))
+        load_w(0, 0, 256, HALF)
+        for mat in range(2):
+            for cg in range(4):
+                if mat + cg > 0:
+                    load_w(mat, cg, 0, HALF)
+
+        m2 = keep.tile([P, P], F32, name="m2")
+        nc.gpsimd.iota(m2[:], pattern=[[2, 64], [0, 2]], base=0, channel_multiplier=0,
+                       allow_small_or_imprecise_dtypes=True)
+        ident = keep.tile([P, P], F32, name="ident")
+        make_identity(nc, ident[:])
+        tokf = keep.tile([P, S], F32, name="tokf")
+        nc.gpsimd.iota(tokf[:], pattern=[[1, TB], [TB, P]], base=0, channel_multiplier=0,
+                       allow_small_or_imprecise_dtypes=True)
+        r8 = keep.tile([P, P], F32, name="r8")
+        nc.gpsimd.iota(r8[:], pattern=[[TB, P]], base=0, channel_multiplier=0, allow_small_or_imprecise_dtypes=True)
+        t8 = keep.tile([P, TB], F32, name="t8")
+        nc.gpsimd.iota(t8[:], pattern=[[1, TB]], base=0, channel_multiplier=0, allow_small_or_imprecise_dtypes=True)
+        ident_bf = keep.tile([P, P], BF16, name="ident_bf")
+        make_identity(nc, ident_bf[:])
+
+        kl = keep.tile([P, P], F32, name="kl")
+        nc.scalar.activation(out=kl[:], in_=m2[:], func=ACT.Ln, scale=1.0 / (1.4 * DK), bias=(0.4 * DK) / (1.4 * DK))
+
+        ones = keep.tile([P, 16], F32, name="ones")
+        nc.vector.memset(ones[:], 1.0)
+        khi = keep.tile([P, P], F32, name="khi")
+        klo = keep.tile([P, P], F32, name="klo")
+        kc = keep.tile([P, 2, P], F32, name="kc")
+        sgv = kc[:, 1, :].rearrange("p (m e) -> p m e", e=2)
+        nc.vector.memset(sgv[:, :, 0:1], 1.0)
+        nc.vector.memset(sgv[:, :, 1:2], -1.0)
+        klov = klo[:].rearrange("p (h l e) -> p h l e", l=8, e=2)
+        onesv = ones[:].rearrange("p (h e) -> p h e", e=2)
+        for i in range(8):
+            nc.vector.tensor_scalar(out=khi[:, 16 * i:16 * i + 16], in0=ones[:], scalar1=10000.0 ** (-8.0 * i / 64.0),
+                                    scalar2=None, op0=ALU.mult)
+            nc.vector.tensor_scalar(out=klov[:, :, i, :], in0=onesv, scalar1=10000.0 ** (-1.0 * i / 64.0),
+                                    scalar2=None, op0=ALU.mult)
+        nc.vector.tensor_tensor(out=kc[:, 0, :], in0=khi[:], in1=klo[:], op=ALU.mult)
+
+        kta = pstp.tile([P, 2, P], F32, tag="tp")
+        for s in range(2):
+            nc.tensor.transpose(kta[:, s, :], kc[:, s, :], ident[:])
+        ktb = pstp.tile([P, P], F32, tag="tp")
+        nc.tensor.transpose(ktb[:], kl[:], ident[:])
+        cst = keep.tile([P, 4], F32, name="cst")
+        nc.vector.tensor_copy(out=cst[:, 0:2], in_=kta[:].rearrange("p s c -> p c s")[:, 0, :])
+        nc.vector.tensor_scalar(out=cst[:, 2:3], in0=cst[:, 0:1], scalar1=1.0 / TWO_PI, scalar2=None, op0=ALU.mult)
+        cl = keep.tile([P, 4], F32, name="cl")
+        nc.vector.tensor_copy(out=cl[:, 0:1], in_=ktb[:, 0:1])
+        nc.vector.tensor_scalar(out=cl[:, 1:2], in0=cl[:, 0:1], scalar1=1.0 / 512.0, scalar2=None, op0=ALU.mult)
+        nc.vector.tensor_scalar(out=cl[:, 2:3], in0=cl[:, 0:1], scalar1=-1.0, scalar2=None, op0=ALU.mult)
+        nc.vector.tensor_scalar(out=cl[:, 3:4], in0=cl[:, 0:1], scalar1=-1.0 / 512.0, scalar2=None, op0=ALU.mult)
+
+        swap = keep.tile([P, P], F32, name="swap")
+        idv = ident[:].rearrange("p (m e) -> p m e", e=2)
+        swv = swap[:].rearrange("p (m e) -> p m e", e=2)
+        nc.vector.tensor_copy(out=swv[:, :, 0:1], in_=idv[:, :, 1:2])
+        nc.vector.tensor_copy(out=swv[:, :, 1:2], in_=idv[:, :, 0:1])
+
+        sq = keep.tile([P, S], F32, name="sq")
+        sk = keep.tile([P, S], F32, name="sk")
+        e2k = keep.tile([P, P], F32, name="e2k")
+        e1k = keep.tile([P, TB], F32, name="e1k")
+        nc.scalar.activation(out=sq[:], in_=tokf[:], func=ACT.Exp, scale=cl[:, 1:2], bias=cl[:, 2:3])
+        nc.scalar.activation(out=e2k[:], in_=r8[:], func=ACT.Exp, scale=cl[:, 3:4], bias=cl[:, 0:1])
+        nc.scalar.activation(out=e1k[:], in_=t8[:], func=ACT.Exp, scale=cl[:, 3:4])
+
+        xg = [[keep.tile([P, HALF, 4], BF16, name="xg%d_%d" % (g, hf), align_bytes=64) for hf in range(2)] for g in range(2)]
+        xc = [[keep.tile([P, HALF], U32, name="xc%d_%d" % (g, hf), align_bytes=64) for hf in range(2)] for g in range(2)]
+        xs = [[keep.tile([P, HALF], U8, name="xs%d_%d" % (g, hf), align_bytes=64) for hf in range(2)] for g in range(2)]
+
+        def x_pair(tp, engines):
+            hf = tp // 2
+            c0 = (tp % 2) * 256
+            for g in range(2):
+                xt = pstp.tile([P, 2, 2, P], F32, tag="tp")
+                for t2 in range(2):
+                    words = x_sb[tp][:, t2, :].bitcast(F32)
+                    for u in range(2):
+                        nc.tensor.transpose(xt[:, t2, u, :], words[:, 256 * g + u:256 * (g + 1):2], ident[:])
+                dst = xg[g][hf][:, c0:c0 + 256, :].rearrange("p c j -> p (c j)").bitcast(F32)
+                dst = dst.rearrange("p (t r u) -> p t r u", t=2, u=2)
+                src = xt[:].rearrange("p t u r -> p t r u")
+                if engines[g] == "v":
+                    nc.vector.tensor_copy(out=dst, in_=src)
+                else:
+                    nc.scalar.copy(out=dst, in_=src)
+
+        def x_quant(tp):
+            hf = tp // 2
+            c0 = (tp % 2) * 256
+            for g in range(2):
+                nc.vector.quantize_mx(out=xc[g][hf][:, c0:c0 + 256].bitcast(FP8X4), scales=xs[g][hf][:, c0:c0 + 256],
+                                      in_=xg[g][hf][:, c0:c0 + 256, :].rearrange("p c j -> p (c j)"))
+
+        sinv = keep.tile([P, S], F32, name="sinv")
+        cosv = keep.tile([P, S], F32, name="cosv")
+        ctab = [keep.tile([P, S], F32, name="ctab%d" % mat) for mat in range(2)]
+        stab = [keep.tile([P, S], F32, name="stab%d" % mat) for mat in range(2)]
+
+        def angles(hf):
+            cols = slice(hf * HALF, (hf + 1) * HALF)
+            t1 = tmp.tile([P, HALF], F32, tag="tmp")
+            nc.vector.tensor_scalar(out=t1[:], in0=tokf[:, cols], scalar1=cst[:, 2:3], scalar2=MAGIC, op0=ALU.mult, op1=ALU.add)
+            ki = tmp.tile([P, HALF], I32, tag="tmp")
+            nc.vector.tensor_scalar(out=ki[:], in0=t1[:], scalar1=-MAGIC, scalar2=None, op0=ALU.add)
+            a = tmp.tile([P, HALF], F32, tag="tmp")
+            nc.vector.tensor_scalar(out=a[:], in0=tokf[:, cols], scalar1=cst[:, 0:1], scalar2=None, op0=ALU.mult)
+            red = tmp.tile([P, HALF], F32, tag="tmp")
+            nc.vector.scalar_tensor_tensor(out=red[:], in0=ki[:], scalar=-TWO_PI, in1=a[:], op0=ALU.mult, op1=ALU.add)
+            nc.scalar.activation(out=sinv[:, cols], in_=red[:], func=ACT.Sin, scale=cst[:, 1:2])
+            ab = tmp.tile([P, HALF], F32, tag="tmp")
+            nc.scalar.activation(out=ab[:], in_=red[:], func=ACT.Abs)
+            nc.scalar.activation(out=cosv[:, cols], in_=ab[:], func=ACT.Sin, scale=-1.0, bias=0.5 * math.pi)
+
+        def tables_q(hf):
+            cols = slice(hf * HALF, (hf + 1) * HALF)
+            nc.vector.tensor_tensor(out=ctab[0][:, cols], in0=cosv[:, cols], in1=sq[:, cols], op=ALU.mult)
+            nc.vector.tensor_tensor(out=stab[0][:, cols], in0=sinv[:, cols], in1=sq[:, cols], op=ALU.mult)
+
+        def tables_k(step):
+            if step < 2:
+                for t in range(4 * step, 4 * step + 4):
+                    nc.gpsimd.tensor_scalar(out=sk[:, t * P:(t + 1) * P], in0=e2k[:], scalar1=e1k[:, t:t + 1], scalar2=0.0,
+                                            op0=ALU.mult, op1=ALU.add)
+            else:
+                cols = slice((step - 2) * HALF, (step - 1) * HALF)
+                nc.gpsimd.tensor_tensor(out=ctab[1][:, cols], in0=cosv[:, cols], in1=sk[:, cols], op=ALU.mult)
+                nc.gpsimd.tensor_tensor(out=stab[1][:, cols], in0=sinv[:, cols], in1=sk[:, cols], op=ALU.mult)
+
+        wc = {}
+        ws = {}
+        acc = {}
+        uv = {}
+
+        def prep(i):
+            mat, h = i // H, i % H
+            c0 = (h % 4) * DK
+            g4 = grp.tile([P, 2, DK, 4], BF16, tag="grp", align_bytes=64)
+            src = wraw[mat][h // 4][:, :, :, c0:c0 + DK].rearrange("p g j c -> p g c j")
+            eng = prep_engine(i)
+            if eng == "v":
+                nc.vector.tensor_copy(out=g4[:], in_=src)
+            elif eng == "g":
+                nc.gpsimd.tensor_scalar(out=g4[:], in0=src, scalar1=1.0, scalar2=0.0, op0=ALU.mult, op1=ALU.add)
+            else:
+                nc.scalar.copy(out=g4[:], in_=src)
+            wc[i] = wcp.tile([P, 2 * DK], U32, tag="wc", name="wc", align_bytes=64)
+            ws[i] = wcp.tile([P, 2 * DK], U8, tag="ws", name="ws", align_bytes=64)
+            nc.vector.quantize_mx(out=wc[i][:].bitcast(FP8X4), scales=ws[i][:], in_=g4[:].rearrange("p g c j -> p (g c j)"))
+
+        def mx(i):
+            acc[i] = [psmx.tile([P, HALF], F32, tag="mx", name="acc%d" % hf) for hf in range(2)]
+            for g in range(2):
+                for hf in range(2):
+                    nc.tensor.matmul_mx(out=acc[i][hf][:],
+                                        lhsT=wc[i][:, g * DK:(g + 1) * DK].bitcast(FP8X4),
+                                        lhsT_scale=ws[i][:, g * DK:(g + 1) * DK],
+                                        rhs=xc[g][hf][:].bitcast(FP8X4), rhs_scale=xs[g][hf][:],
+                                        start=(g == 0), stop=(g == 1))
+
+        def rot(i, hf):
+            mat = i // H
+            cols = slice(hf * HALF, (hf + 1) * HALF)
+            if g_rot(i, hf):
+                t = gvp.tile([P, HALF], F32, tag="t")
+                u = gvp.tile([P, HALF], F32, tag="ug")
+                v = gvp.tile([P, HALF], F32, tag="vg")
+                nc.scalar.activation(out=t[:], in_=acc[i][hf][:], func=ACT.Identity, bias=biasT[:, i:i + 1])
+                nc.gpsimd.tensor_tensor(out=u[:], in0=t[:], in1=ctab[mat][:, cols], op=ALU.mult)
+                nc.gpsimd.tensor_tensor(out=v[:], in0=t[:], in1=stab[mat][:, cols], op=ALU.mult)
+            else:
+                u = uvp.tile([P, HALF], F32, tag="u")
+                v = uvp.tile([P, HALF], F32, tag="v")
+                nc.vector.scalar_tensor_tensor(out=u[:], in0=acc[i][hf][:], scalar=biasT[:, i:i + 1], in1=ctab[mat][:, cols],
+                                               op0=ALU.add, op1=ALU.mult)
+                nc.vector.scalar_tensor_tensor(out=v[:], in0=acc[i][hf][:], scalar=biasT[:, i:i + 1], in1=stab[mat][:, cols],
+                                               op0=ALU.add, op1=ALU.mult)
+            uv[(i, hf)] = (u, v)
+
+        def back(i, hf):
+            mat, h = i // H, i % H
+            u, v = uv[(i, hf)]
+            o = pstp.tile([P, 4, DK], F32, tag="tp")
+            for tl in range(4):
+                blk = slice(tl * P, (tl + 1) * P)
+                nc.tensor.matmul(out=o[:, tl, :], lhsT=u[:, blk], rhs=ident[:], is_transpose=True, start=True, stop=False)
+                nc.tensor.matmul(out=o[:, tl, :], lhsT=v[:, blk], rhs=swap[:], is_transpose=True, start=False, stop=True)
+            osb = outp.tile([P, 4, DK], F32, tag="o")
+            nc.scalar.copy(out=osb[:], in_=o[:])
+            nc.sync.dma_start(out=outv[mat][h][:, 4 * hf:4 * hf + 4, :], in_=osb[:])
+
+        angles(0)
+        x_pair(0, "vv")
+        x_quant(0)
+        x_pair(1, "vv")
+        x_quant(1)
+        bt_ps = pstp.tile([P, P], BF16, tag="tp")
+        nc.tensor.transpose(bt_ps[:], btile[:], ident_bf[:])
+        biasT = keep.tile([P, 2 * H], F32, name="biasT")
+        nc.vector.tensor_copy(out=biasT[:], in_=bt_ps[:, 0:2 * H])
+        prep(0)
+        angles(1)
+        tables_q(0)
+        x_pair(2, "ss")
+        x_quant(2)
+        x_pair(3, "ss")
+        x_quant(3)
+        prep(1)
+        tables_q(1)
+        mx(0)
+        late = []
+        for i in range(NT + 1):
+            if i + 2 < NT:
+                prep(i + 2)
+            if i + 1 < NT:
+                mx(i + 1)
+            if 2 <= i < 6:
+                tables_k(i - 2)
+            now = late
+            late = []
+            if i < NT:
+                for hf in range(2):
+                    rot(i, hf)
+                    if g_rot(i, hf):
+                        late.append((i, hf))
+                    else:
+                        now.append((i, hf))
+            for b in now:
+                back(b[0], b[1])

@@ -28,21 +28,19 @@ NT = 2 * H
 
 
 def g_rot(i, hf):
-    return hf == 1 and i % 2 == 1
-
-
-def prep_engine(i):
-    return "v" if i < 2 else ("g" if i % 3 == 2 else "s")
+    return hf == 1 and i % 2 == 1 and i < 28
 
 
 def tile_gatedmultiscaleretentionlayer_pa_kernel(tc, x, Wq, bq, Wk, bk, out_0, out_1):
     nc = tc.nc
     with ExitStack() as ctx:
+        ctx.enter_context(tc.manual_schedule())
         keep = ctx.enter_context(tc.tile_pool(name="keep", bufs=1))
-        tmp = ctx.enter_context(tc.tile_pool(name="tmp", bufs=5))
-        grp = ctx.enter_context(tc.tile_pool(name="grp", bufs=4))
-        wcp = ctx.enter_context(tc.tile_pool(name="wcp", bufs=5))
-        uvp = ctx.enter_context(tc.tile_pool(name="uvp", bufs=4))
+        wrp = ctx.enter_context(tc.tile_pool(name="wrp", bufs=4))
+        tmp = ctx.enter_context(tc.tile_pool(name="tmp", bufs=8))
+        grp = ctx.enter_context(tc.tile_pool(name="grp", bufs=3))
+        wcp = ctx.enter_context(tc.tile_pool(name="wcp", bufs=3))
+        uvp = ctx.enter_context(tc.tile_pool(name="uvp", bufs=5))
         gvp = ctx.enter_context(tc.tile_pool(name="gvp", bufs=2))
         outp = ctx.enter_context(tc.tile_pool(name="outp", bufs=6))
         psmx = ctx.enter_context(tc.psum_pool(name="psmx", bufs=4))
@@ -53,29 +51,29 @@ def tile_gatedmultiscaleretentionlayer_pa_kernel(tc, x, Wq, bq, Wk, bk, out_0, o
         outv = [o.rearrange("b h (r t) f -> (b h) r t f", t=TB) for o in (out_0, out_1)]
 
         x_sb = [keep.tile([P, 2, D], BF16, name="x_sb%d" % tp) for tp in range(4)]
-        wraw = [[keep.tile([P, 2, 4, HALF], BF16, name="wraw%d_%d" % (mat, cg)) for cg in range(4)] for mat in range(2)]
+        wraw = {}
         btile = keep.tile([P, P], BF16, name="btile")
         nc.vector.memset(btile[:], 0.0)
 
         def load_x(tp):
             nc.sync.dma_start(out=x_sb[tp][:], in_=xv[:, 2 * tp:2 * tp + 2, :])
 
-        def load_w(mat, cg, c0, c1):
+        def load_w(q, c0, c1):
+            if c0 == 0:
+                wraw[q] = wrp.tile([P, 2, 4, HALF], BF16, tag="wraw", name="wraw")
             for g in range(2):
-                nc.sync.dma_start(out=wraw[mat][cg][:, g, :, c0:c1], in_=wv[mat][g, :, :, cg * HALF + c0:cg * HALF + c1])
+                nc.sync.dma_start(out=wraw[q][:, g, :, c0:c1], in_=wv[q // 4][g, :, :, (q % 4) * HALF + c0:(q % 4) * HALF + c1])
 
         load_x(0)
         load_x(1)
-        load_w(0, 0, 0, 256)
+        load_w(0, 0, 256)
         load_x(2)
         load_x(3)
         nc.sync.dma_start(out=btile[0:H, :], in_=bq.rearrange("(h c) -> h c", c=DK))
         nc.sync.dma_start(out=btile[H:2 * H, :], in_=bk.rearrange("(h c) -> h c", c=DK))
-        load_w(0, 0, 256, HALF)
-        for mat in range(2):
-            for cg in range(4):
-                if mat + cg > 0:
-                    load_w(mat, cg, 0, HALF)
+        load_w(0, 256, HALF)
+        load_w(1, 0, HALF)
+        load_w(2, 0, HALF)
 
         m2 = keep.tile([P, P], F32, name="m2")
         nc.gpsimd.iota(m2[:], pattern=[[2, 64], [0, 2]], base=0, channel_multiplier=0,
@@ -117,6 +115,11 @@ def tile_gatedmultiscaleretentionlayer_pa_kernel(tc, x, Wq, bq, Wk, bk, out_0, o
             nc.tensor.transpose(kta[:, s, :], kc[:, s, :], ident[:])
         ktb = pstp.tile([P, P], F32, tag="tp")
         nc.tensor.transpose(ktb[:], kl[:], ident[:])
+        swap = keep.tile([P, P], F32, name="swap")
+        idv = ident[:].rearrange("p (m e) -> p m e", e=2)
+        swv = swap[:].rearrange("p (m e) -> p m e", e=2)
+        nc.vector.tensor_copy(out=swv[:, :, 0:1], in_=idv[:, :, 1:2])
+        nc.vector.tensor_copy(out=swv[:, :, 1:2], in_=idv[:, :, 0:1])
         cst = keep.tile([P, 4], F32, name="cst")
         nc.vector.tensor_copy(out=cst[:, 0:2], in_=kta[:].rearrange("p s c -> p c s")[:, 0, :])
         nc.vector.tensor_scalar(out=cst[:, 2:3], in0=cst[:, 0:1], scalar1=1.0 / TWO_PI, scalar2=None, op0=ALU.mult)
@@ -125,12 +128,6 @@ def tile_gatedmultiscaleretentionlayer_pa_kernel(tc, x, Wq, bq, Wk, bk, out_0, o
         nc.vector.tensor_scalar(out=cl[:, 1:2], in0=cl[:, 0:1], scalar1=1.0 / 512.0, scalar2=None, op0=ALU.mult)
         nc.vector.tensor_scalar(out=cl[:, 2:3], in0=cl[:, 0:1], scalar1=-1.0, scalar2=None, op0=ALU.mult)
         nc.vector.tensor_scalar(out=cl[:, 3:4], in0=cl[:, 0:1], scalar1=-1.0 / 512.0, scalar2=None, op0=ALU.mult)
-
-        swap = keep.tile([P, P], F32, name="swap")
-        idv = ident[:].rearrange("p (m e) -> p m e", e=2)
-        swv = swap[:].rearrange("p (m e) -> p m e", e=2)
-        nc.vector.tensor_copy(out=swv[:, :, 0:1], in_=idv[:, :, 1:2])
-        nc.vector.tensor_copy(out=swv[:, :, 1:2], in_=idv[:, :, 0:1])
 
         sq = keep.tile([P, S], F32, name="sq")
         sk = keep.tile([P, S], F32, name="sk")
@@ -172,8 +169,9 @@ def tile_gatedmultiscaleretentionlayer_pa_kernel(tc, x, Wq, bq, Wk, bk, out_0, o
         cosv = keep.tile([P, S], F32, name="cosv")
         ctab = [keep.tile([P, S], F32, name="ctab%d" % mat) for mat in range(2)]
         stab = [keep.tile([P, S], F32, name="stab%d" % mat) for mat in range(2)]
+        red = {}
 
-        def angles(hf):
+        def angles_v(hf):
             cols = slice(hf * HALF, (hf + 1) * HALF)
             t1 = tmp.tile([P, HALF], F32, tag="tmp")
             nc.vector.tensor_scalar(out=t1[:], in0=tokf[:, cols], scalar1=cst[:, 2:3], scalar2=MAGIC, op0=ALU.mult, op1=ALU.add)
@@ -181,17 +179,20 @@ def tile_gatedmultiscaleretentionlayer_pa_kernel(tc, x, Wq, bq, Wk, bk, out_0, o
             nc.vector.tensor_scalar(out=ki[:], in0=t1[:], scalar1=-MAGIC, scalar2=None, op0=ALU.add)
             a = tmp.tile([P, HALF], F32, tag="tmp")
             nc.vector.tensor_scalar(out=a[:], in0=tokf[:, cols], scalar1=cst[:, 0:1], scalar2=None, op0=ALU.mult)
-            red = tmp.tile([P, HALF], F32, tag="tmp")
-            nc.vector.scalar_tensor_tensor(out=red[:], in0=ki[:], scalar=-TWO_PI, in1=a[:], op0=ALU.mult, op1=ALU.add)
-            nc.scalar.activation(out=sinv[:, cols], in_=red[:], func=ACT.Sin, scale=cst[:, 1:2])
-            ab = tmp.tile([P, HALF], F32, tag="tmp")
-            nc.scalar.activation(out=ab[:], in_=red[:], func=ACT.Abs)
+            red[hf] = tmp.tile([P, HALF], F32, tag="tmp", name="red")
+            nc.vector.scalar_tensor_tensor(out=red[hf][:], in0=ki[:], scalar=-TWO_PI, in1=a[:], op0=ALU.mult, op1=ALU.add)
+
+        def angles_s(hf):
+            cols = slice(hf * HALF, (hf + 1) * HALF)
+            nc.scalar.activation(out=sinv[:, cols], in_=red[hf][:], func=ACT.Sin, scale=cst[:, 1:2])
+            ab = keep.tile([P, HALF], F32, name="ab%d" % hf)
+            nc.scalar.activation(out=ab[:], in_=red[hf][:], func=ACT.Abs)
             nc.scalar.activation(out=cosv[:, cols], in_=ab[:], func=ACT.Sin, scale=-1.0, bias=0.5 * math.pi)
 
-        def tables_q(hf):
+        def tables_q(hf, eng):
             cols = slice(hf * HALF, (hf + 1) * HALF)
-            nc.vector.tensor_tensor(out=ctab[0][:, cols], in0=cosv[:, cols], in1=sq[:, cols], op=ALU.mult)
-            nc.vector.tensor_tensor(out=stab[0][:, cols], in0=sinv[:, cols], in1=sq[:, cols], op=ALU.mult)
+            eng.tensor_tensor(out=ctab[0][:, cols], in0=cosv[:, cols], in1=sq[:, cols], op=ALU.mult)
+            eng.tensor_tensor(out=stab[0][:, cols], in0=sinv[:, cols], in1=sq[:, cols], op=ALU.mult)
 
         def tables_k(step):
             if step < 2:
@@ -203,103 +204,146 @@ def tile_gatedmultiscaleretentionlayer_pa_kernel(tc, x, Wq, bq, Wk, bk, out_0, o
                 nc.gpsimd.tensor_tensor(out=ctab[1][:, cols], in0=cosv[:, cols], in1=sk[:, cols], op=ALU.mult)
                 nc.gpsimd.tensor_tensor(out=stab[1][:, cols], in0=sinv[:, cols], in1=sk[:, cols], op=ALU.mult)
 
+        unit_of = {0: (0, 1), 1: (1, 1)}
+        for a in range(2, NT, 2):
+            unit_of[a] = (a, 2)
+            unit_of[a + 1] = (a, 2)
+        g4 = {}
         wc = {}
         ws = {}
         acc = {}
         uv = {}
+        tsb = {}
+        otp = {}
 
-        def prep(i):
-            mat, h = i // H, i % H
-            c0 = (h % 4) * DK
-            g4 = grp.tile([P, 2, DK, 4], BF16, tag="grp", align_bytes=64)
-            src = wraw[mat][h // 4][:, :, :, c0:c0 + DK].rearrange("p g j c -> p g c j")
-            eng = prep_engine(i)
+        def inter(i, eng):
+            a, n = unit_of[i]
+            if i == a:
+                g4[a] = grp.tile([P, 2, n * DK, 4], BF16, tag="grp", name="g4", align_bytes=64)
+            c0 = (i % 4) * DK
+            src = wraw[i // 4][:, :, :, c0:c0 + DK].rearrange("p g j c -> p g c j")
+            dst = g4[a][:, :, (i - a) * DK:(i - a + 1) * DK, :]
             if eng == "v":
-                nc.vector.tensor_copy(out=g4[:], in_=src)
+                nc.vector.tensor_copy(out=dst, in_=src)
             elif eng == "g":
-                nc.gpsimd.tensor_scalar(out=g4[:], in0=src, scalar1=1.0, scalar2=0.0, op0=ALU.mult, op1=ALU.add)
+                nc.gpsimd.tensor_scalar(out=dst, in0=src, scalar1=1.0, scalar2=0.0, op0=ALU.mult, op1=ALU.add)
             else:
-                nc.scalar.copy(out=g4[:], in_=src)
-            wc[i] = wcp.tile([P, 2 * DK], U32, tag="wc", name="wc", align_bytes=64)
-            ws[i] = wcp.tile([P, 2 * DK], U8, tag="ws", name="ws", align_bytes=64)
-            nc.vector.quantize_mx(out=wc[i][:].bitcast(FP8X4), scales=ws[i][:], in_=g4[:].rearrange("p g c j -> p (g c j)"))
+                nc.scalar.copy(out=dst, in_=src)
+
+        def quant(a):
+            n = unit_of[a][1]
+            wc[a] = wcp.tile([P, 2 * n * DK], U32, tag="wc", name="wc", align_bytes=64)
+            ws[a] = wcp.tile([P, 2 * n * DK], U8, tag="ws", name="ws", align_bytes=64)
+            nc.vector.quantize_mx(out=wc[a][:].bitcast(FP8X4), scales=ws[a][:], in_=g4[a][:].rearrange("p g c j -> p (g c j)"))
 
         def mx(i):
+            a, n = unit_of[i]
             acc[i] = [psmx.tile([P, HALF], F32, tag="mx", name="acc%d" % hf) for hf in range(2)]
-            for g in range(2):
-                for hf in range(2):
+            for hf in range(2):
+                for g in range(2):
+                    c0 = (g * n + i - a) * DK
                     nc.tensor.matmul_mx(out=acc[i][hf][:],
-                                        lhsT=wc[i][:, g * DK:(g + 1) * DK].bitcast(FP8X4),
-                                        lhsT_scale=ws[i][:, g * DK:(g + 1) * DK],
+                                        lhsT=wc[a][:, c0:c0 + DK].bitcast(FP8X4), lhsT_scale=ws[a][:, c0:c0 + DK],
                                         rhs=xc[g][hf][:].bitcast(FP8X4), rhs_scale=xs[g][hf][:],
                                         start=(g == 0), stop=(g == 1))
 
-        def rot(i, hf):
+        def rot_v(i, hf):
             mat = i // H
             cols = slice(hf * HALF, (hf + 1) * HALF)
-            if g_rot(i, hf):
-                t = gvp.tile([P, HALF], F32, tag="t")
-                u = gvp.tile([P, HALF], F32, tag="ug")
-                v = gvp.tile([P, HALF], F32, tag="vg")
-                nc.scalar.activation(out=t[:], in_=acc[i][hf][:], func=ACT.Identity, bias=biasT[:, i:i + 1])
-                nc.gpsimd.tensor_tensor(out=u[:], in0=t[:], in1=ctab[mat][:, cols], op=ALU.mult)
-                nc.gpsimd.tensor_tensor(out=v[:], in0=t[:], in1=stab[mat][:, cols], op=ALU.mult)
-            else:
-                u = uvp.tile([P, HALF], F32, tag="u")
-                v = uvp.tile([P, HALF], F32, tag="v")
-                nc.vector.scalar_tensor_tensor(out=u[:], in0=acc[i][hf][:], scalar=biasT[:, i:i + 1], in1=ctab[mat][:, cols],
-                                               op0=ALU.add, op1=ALU.mult)
-                nc.vector.scalar_tensor_tensor(out=v[:], in0=acc[i][hf][:], scalar=biasT[:, i:i + 1], in1=stab[mat][:, cols],
-                                               op0=ALU.add, op1=ALU.mult)
+            u = uvp.tile([P, HALF], F32, tag="u")
+            v = uvp.tile([P, HALF], F32, tag="v")
+            nc.vector.scalar_tensor_tensor(out=u[:], in0=acc[i][hf][:], scalar=biasT[:, i:i + 1], in1=ctab[mat][:, cols],
+                                           op0=ALU.add, op1=ALU.mult)
+            nc.vector.scalar_tensor_tensor(out=v[:], in0=acc[i][hf][:], scalar=biasT[:, i:i + 1], in1=stab[mat][:, cols],
+                                           op0=ALU.add, op1=ALU.mult)
+            uv[(i, hf)] = (u, v)
+
+        def rot_s(i, hf):
+            tsb[(i, hf)] = gvp.tile([P, HALF], F32, tag="t", name="tsb")
+            nc.scalar.activation(out=tsb[(i, hf)][:], in_=acc[i][hf][:], func=ACT.Identity, bias=biasT[:, i:i + 1])
+
+        def rot_g(i, hf):
+            mat = i // H
+            cols = slice(hf * HALF, (hf + 1) * HALF)
+            u = gvp.tile([P, HALF], F32, tag="ug")
+            v = gvp.tile([P, HALF], F32, tag="vg")
+            nc.gpsimd.tensor_tensor(out=u[:], in0=tsb[(i, hf)][:], in1=ctab[mat][:, cols], op=ALU.mult)
+            nc.gpsimd.tensor_tensor(out=v[:], in0=tsb[(i, hf)][:], in1=stab[mat][:, cols], op=ALU.mult)
             uv[(i, hf)] = (u, v)
 
         def back(i, hf):
-            mat, h = i // H, i % H
             u, v = uv[(i, hf)]
             o = pstp.tile([P, 4, DK], F32, tag="tp")
             for tl in range(4):
                 blk = slice(tl * P, (tl + 1) * P)
                 nc.tensor.matmul(out=o[:, tl, :], lhsT=u[:, blk], rhs=ident[:], is_transpose=True, start=True, stop=False)
                 nc.tensor.matmul(out=o[:, tl, :], lhsT=v[:, blk], rhs=swap[:], is_transpose=True, start=False, stop=True)
+            otp[(i, hf)] = o
+
+        def leave(i, hf, eng):
+            mat, h = i // H, i % H
             osb = outp.tile([P, 4, DK], F32, tag="o")
-            nc.scalar.copy(out=osb[:], in_=o[:])
+            if eng == "v":
+                nc.vector.tensor_copy(out=osb[:], in_=otp[(i, hf)][:])
+            else:
+                nc.scalar.copy(out=osb[:], in_=otp[(i, hf)][:])
             nc.sync.dma_start(out=outv[mat][h][:, 4 * hf:4 * hf + 4, :], in_=osb[:])
 
-        angles(0)
+        angles_v(0)
+        angles_s(0)
+        angles_v(1)
         x_pair(0, "vv")
         x_quant(0)
         x_pair(1, "vv")
         x_quant(1)
+        angles_s(1)
+        inter(0, "v")
+        quant(0)
         bt_ps = pstp.tile([P, P], BF16, tag="tp")
         nc.tensor.transpose(bt_ps[:], btile[:], ident_bf[:])
         biasT = keep.tile([P, 2 * H], F32, name="biasT")
         nc.vector.tensor_copy(out=biasT[:], in_=bt_ps[:, 0:2 * H])
-        prep(0)
-        angles(1)
-        tables_q(0)
         x_pair(2, "ss")
-        x_quant(2)
         x_pair(3, "ss")
+        tables_q(0, nc.vector)
+        tables_q(1, nc.gpsimd)
+        inter(1, "s")
+        x_quant(2)
         x_quant(3)
-        prep(1)
-        tables_q(1)
-        mx(0)
-        late = []
-        for i in range(NT + 1):
-            if i + 2 < NT:
-                prep(i + 2)
-            if i + 1 < NT:
-                mx(i + 1)
-            if 2 <= i < 6:
-                tables_k(i - 2)
-            now = late
-            late = []
-            if i < NT:
+        quant(1)
+        inter(2, "g")
+        inter(3, "g")
+
+        done = []
+        for s in range(NT + 6):
+            if s < NT:
+                mx(s)
+            if 0 <= s - 1 < NT:
                 for hf in range(2):
-                    rot(i, hf)
-                    if g_rot(i, hf):
-                        late.append((i, hf))
-                    else:
-                        now.append((i, hf))
-            for b in now:
+                    if g_rot(s - 1, hf):
+                        rot_s(s - 1, hf)
+            if 0 <= s - 1 < NT:
+                for hf in range(2):
+                    if not g_rot(s - 1, hf):
+                        rot_v(s - 1, hf)
+            if 0 <= s - 2 < NT:
+                for hf in range(2):
+                    if g_rot(s - 2, hf):
+                        rot_g(s - 2, hf)
+            if s % 2 == 0 and s + 2 < NT:
+                quant(s + 2)
+            for n, b in enumerate(done):
+                leave(b[0], b[1], "v" if (s % 2 == 0 and n == 1) else "s")
+            done = []
+            if 0 <= s - 2 < NT:
+                done.extend([(s - 2, hf) for hf in range(2) if not g_rot(s - 2, hf)])
+            if 0 <= s - 4 < NT:
+                done.extend([(s - 4, hf) for hf in range(2) if g_rot(s - 4, hf)])
+            for b in done:
                 back(b[0], b[1])
+            if s + 4 < NT:
+                inter(s + 4, "s")
+            if s % 4 == 2 and 3 <= (s + 10) // 4 < 8:
+                load_w((s + 10) // 4, 0, HALF)
+            if 4 <= s < 8:
+                tables_k(s - 4)

@@ -28,7 +28,7 @@ NT = 2 * H
 
 
 def g_rot(i, hf):
-    return hf == 1 and i % 2 == 1 and i < 28
+    return hf == 1 and i % 2 == 1
 
 
 def tile_gatedmultiscaleretentionlayer_pa_kernel(tc, x, Wq, bq, Wk, bk, out_0, out_1):
@@ -40,7 +40,7 @@ def tile_gatedmultiscaleretentionlayer_pa_kernel(tc, x, Wq, bq, Wk, bk, out_0, o
         tmp = ctx.enter_context(tc.tile_pool(name="tmp", bufs=8))
         grp = ctx.enter_context(tc.tile_pool(name="grp", bufs=3))
         wcp = ctx.enter_context(tc.tile_pool(name="wcp", bufs=3))
-        uvp = ctx.enter_context(tc.tile_pool(name="uvp", bufs=5))
+        uvp = ctx.enter_context(tc.tile_pool(name="uvp", bufs=6))
         gvp = ctx.enter_context(tc.tile_pool(name="gvp", bufs=2))
         outp = ctx.enter_context(tc.tile_pool(name="outp", bufs=6))
         psmx = ctx.enter_context(tc.psum_pool(name="psmx", bufs=4))
@@ -314,36 +314,31 @@ def tile_gatedmultiscaleretentionlayer_pa_kernel(tc, x, Wq, bq, Wk, bk, out_0, o
         inter(2, "g")
         inter(3, "g")
 
-        done = []
-        for s in range(NT + 6):
-            if s < NT:
-                mx(s)
-            if 0 <= s - 1 < NT:
-                for hf in range(2):
-                    if g_rot(s - 1, hf):
-                        rot_s(s - 1, hf)
-            if 0 <= s - 1 < NT:
-                for hf in range(2):
-                    if not g_rot(s - 1, hf):
-                        rot_v(s - 1, hf)
-            if 0 <= s - 2 < NT:
-                for hf in range(2):
-                    if g_rot(s - 2, hf):
-                        rot_g(s - 2, hf)
-            if s % 2 == 0 and s + 2 < NT:
-                quant(s + 2)
-            for n, b in enumerate(done):
-                leave(b[0], b[1], "v" if (s % 2 == 0 and n == 1) else "s")
-            done = []
-            if 0 <= s - 2 < NT:
-                done.extend([(s - 2, hf) for hf in range(2) if not g_rot(s - 2, hf)])
-            if 0 <= s - 4 < NT:
-                done.extend([(s - 4, hf) for hf in range(2) if g_rot(s - 4, hf)])
-            for b in done:
-                back(b[0], b[1])
-            if s + 4 < NT:
-                inter(s + 4, "s")
-            if s % 4 == 2 and 3 <= (s + 10) // 4 < 8:
-                load_w((s + 10) // 4, 0, HALF)
-            if 4 <= s < 8:
-                tables_k(s - 4)
+        NP = NT // 2
+        for p in range(NP + 1):
+            if p + 1 < NP:
+                quant(2 * p + 2)
+            if p < NP:
+                mx(2 * p)
+                mx(2 * p + 1)
+                if 2 * p + 5 < NT:
+                    inter(2 * p + 4, "s")
+                    inter(2 * p + 5, "g")
+                banks = [(2 * p, 0), (2 * p, 1), (2 * p + 1, 0), (2 * p + 1, 1)]
+                for b in banks:
+                    if not g_rot(b[0], b[1]):
+                        rot_v(b[0], b[1])
+                for b in banks:
+                    if g_rot(b[0], b[1]):
+                        rot_s(b[0], b[1])
+                        rot_g(b[0], b[1])
+            if p > 0:
+                banks = [(2 * p - 2, 0), (2 * p - 2, 1), (2 * p - 1, 0), (2 * p - 1, 1)]
+                for b in banks:
+                    back(b[0], b[1])
+                for n, b in enumerate(banks):
+                    leave(b[0], b[1], "v" if (p == NP and n % 2 == 0) else "s")
+            if p % 2 == 1 and 3 <= (p + 5) // 2 < 8:
+                load_w((p + 5) // 2, 0, HALF)
+            if 2 <= p < 6:
+                tables_k(p - 2)

@@ -25,10 +25,13 @@ HALF = 512
 TWO_PI = 2.0 * math.pi
 MAGIC = 12582912.0
 NT = 2 * H
+PATH = ("B", "A")
+NB = PATH.count("B")
+NA = PATH.count("A")
 
 
-def g_rot(i, hf):
-    return hf == 1 and i % 2 == 1
+def inter_engine(i):
+    return "g" if i % 2 == 1 else "s"
 
 
 def tile_gatedmultiscaleretentionlayer_pa_kernel(tc, x, Wq, bq, Wk, bk, out_0, out_1):
@@ -37,12 +40,11 @@ def tile_gatedmultiscaleretentionlayer_pa_kernel(tc, x, Wq, bq, Wk, bk, out_0, o
         ctx.enter_context(tc.manual_schedule())
         keep = ctx.enter_context(tc.tile_pool(name="keep", bufs=1))
         wrp = ctx.enter_context(tc.tile_pool(name="wrp", bufs=4))
-        tmp = ctx.enter_context(tc.tile_pool(name="tmp", bufs=8))
         grp = ctx.enter_context(tc.tile_pool(name="grp", bufs=3))
         wcp = ctx.enter_context(tc.tile_pool(name="wcp", bufs=3))
-        uvp = ctx.enter_context(tc.tile_pool(name="uvp", bufs=6))
-        gvp = ctx.enter_context(tc.tile_pool(name="gvp", bufs=2))
-        outp = ctx.enter_context(tc.tile_pool(name="outp", bufs=6))
+        bp = ctx.enter_context(tc.tile_pool(name="bp", bufs=max(3 * NB, 1)))
+        ap = ctx.enter_context(tc.tile_pool(name="ap", bufs=max(3 * NA, 1)))
+        outp = ctx.enter_context(tc.tile_pool(name="outp", bufs=8))
         psmx = ctx.enter_context(tc.psum_pool(name="psmx", bufs=4))
         pstp = ctx.enter_context(tc.psum_pool(name="pstp", bufs=4))
 
@@ -80,13 +82,14 @@ def tile_gatedmultiscaleretentionlayer_pa_kernel(tc, x, Wq, bq, Wk, bk, out_0, o
                        allow_small_or_imprecise_dtypes=True)
         ident = keep.tile([P, P], F32, name="ident")
         make_identity(nc, ident[:])
-        tokf = keep.tile([P, S], F32, name="tokf")
-        nc.gpsimd.iota(tokf[:], pattern=[[1, TB], [TB, P]], base=0, channel_multiplier=0,
-                       allow_small_or_imprecise_dtypes=True)
-        r8 = keep.tile([P, P], F32, name="r8")
-        nc.gpsimd.iota(r8[:], pattern=[[TB, P]], base=0, channel_multiplier=0, allow_small_or_imprecise_dtypes=True)
-        t8 = keep.tile([P, TB], F32, name="t8")
-        nc.gpsimd.iota(t8[:], pattern=[[1, TB]], base=0, channel_multiplier=0, allow_small_or_imprecise_dtypes=True)
+        tok_b = {}
+        for hf in range(2):
+            if PATH[hf] == "B":
+                tok_b[hf] = keep.tile([P, HALF], F32, name="tok_b%d" % hf)
+                nc.gpsimd.iota(tok_b[hf][:], pattern=[[1, 4], [TB, P]], base=4 * hf, channel_multiplier=0,
+                               allow_small_or_imprecise_dtypes=True)
+        tok_a = keep.tile([P, TB], F32, name="tok_a")
+        nc.gpsimd.iota(tok_a[:], pattern=[[1, TB]], base=0, channel_multiplier=TB, allow_small_or_imprecise_dtypes=True)
         ident_bf = keep.tile([P, P], BF16, name="ident_bf")
         make_identity(nc, ident_bf[:])
 
@@ -110,32 +113,80 @@ def tile_gatedmultiscaleretentionlayer_pa_kernel(tc, x, Wq, bq, Wk, bk, out_0, o
                                     scalar2=None, op0=ALU.mult)
         nc.vector.tensor_tensor(out=kc[:, 0, :], in0=khi[:], in1=klo[:], op=ALU.mult)
 
-        kta = pstp.tile([P, 2, P], F32, tag="tp")
-        for s in range(2):
-            nc.tensor.transpose(kta[:, s, :], kc[:, s, :], ident[:])
-        ktb = pstp.tile([P, P], F32, tag="tp")
-        nc.tensor.transpose(ktb[:], kl[:], ident[:])
-        swap = keep.tile([P, P], F32, name="swap")
-        idv = ident[:].rearrange("p (m e) -> p m e", e=2)
-        swv = swap[:].rearrange("p (m e) -> p m e", e=2)
-        nc.vector.tensor_copy(out=swv[:, :, 0:1], in_=idv[:, :, 1:2])
-        nc.vector.tensor_copy(out=swv[:, :, 1:2], in_=idv[:, :, 0:1])
         cst = keep.tile([P, 4], F32, name="cst")
-        nc.vector.tensor_copy(out=cst[:, 0:2], in_=kta[:].rearrange("p s c -> p c s")[:, 0, :])
-        nc.vector.tensor_scalar(out=cst[:, 2:3], in0=cst[:, 0:1], scalar1=1.0 / TWO_PI, scalar2=None, op0=ALU.mult)
         cl = keep.tile([P, 4], F32, name="cl")
-        nc.vector.tensor_copy(out=cl[:, 0:1], in_=ktb[:, 0:1])
-        nc.vector.tensor_scalar(out=cl[:, 1:2], in0=cl[:, 0:1], scalar1=1.0 / 512.0, scalar2=None, op0=ALU.mult)
-        nc.vector.tensor_scalar(out=cl[:, 2:3], in0=cl[:, 0:1], scalar1=-1.0, scalar2=None, op0=ALU.mult)
-        nc.vector.tensor_scalar(out=cl[:, 3:4], in0=cl[:, 0:1], scalar1=-1.0 / 512.0, scalar2=None, op0=ALU.mult)
+        swap = keep.tile([P, P], F32, name="swap")
+        wsgn = keep.tile([P, P], F32, name="wsgn")
+        pw_a = keep.tile([P, TB], F32, name="pw_a")
+        if NA > 0:
+            nc.vector.scalar_tensor_tensor(out=wsgn[:], in0=kc[:, 0, :], scalar=-1.0, in1=kc[:, 1, :], op0=ALU.mult, op1=ALU.mult)
+            nc.vector.tensor_scalar(out=pw_a[:], in0=tok_a[:], scalar1=-512.0, scalar2=1.0 / 512.0, op0=ALU.add, op1=ALU.mult)
+        if NB > 0:
+            kta = pstp.tile([P, 2, P], F32, tag="tp")
+            for s in range(2):
+                nc.tensor.transpose(kta[:, s, :], kc[:, s, :], ident[:])
+            ktb = pstp.tile([P, P], F32, tag="tp")
+            nc.tensor.transpose(ktb[:], kl[:], ident[:])
+            idv = ident[:].rearrange("p (m e) -> p m e", e=2)
+            swv = swap[:].rearrange("p (m e) -> p m e", e=2)
+            nc.vector.tensor_copy(out=swv[:, :, 0:1], in_=idv[:, :, 1:2])
+            nc.vector.tensor_copy(out=swv[:, :, 1:2], in_=idv[:, :, 0:1])
+            nc.vector.tensor_copy(out=cst[:, 0:2], in_=kta[:].rearrange("p s c -> p c s")[:, 0, :])
+            nc.vector.tensor_scalar(out=cst[:, 2:3], in0=cst[:, 0:1], scalar1=1.0 / TWO_PI, scalar2=None, op0=ALU.mult)
+            nc.vector.tensor_copy(out=cl[:, 0:1], in_=ktb[:, 0:1])
+            nc.vector.tensor_scalar(out=cl[:, 1:2], in0=cl[:, 0:1], scalar1=1.0 / 512.0, scalar2=None, op0=ALU.mult)
+            nc.vector.tensor_scalar(out=cl[:, 2:3], in0=cl[:, 0:1], scalar1=-1.0, scalar2=None, op0=ALU.mult)
+            nc.vector.tensor_scalar(out=cl[:, 3:4], in0=cl[:, 0:1], scalar1=-1.0 / 512.0, scalar2=None, op0=ALU.mult)
 
-        sq = keep.tile([P, S], F32, name="sq")
-        sk = keep.tile([P, S], F32, name="sk")
-        e2k = keep.tile([P, P], F32, name="e2k")
-        e1k = keep.tile([P, TB], F32, name="e1k")
-        nc.scalar.activation(out=sq[:], in_=tokf[:], func=ACT.Exp, scale=cl[:, 1:2], bias=cl[:, 2:3])
-        nc.scalar.activation(out=e2k[:], in_=r8[:], func=ACT.Exp, scale=cl[:, 3:4], bias=cl[:, 0:1])
-        nc.scalar.activation(out=e1k[:], in_=t8[:], func=ACT.Exp, scale=cl[:, 3:4])
+        scl = [[keep.tile([P, HALF], F32, name="scl%d_%d" % (mat, hf)) for hf in range(2)] for mat in range(2)]
+        sinv = [keep.tile([P, HALF], F32, name="sinv%d" % hf) for hf in range(2)]
+        cosv = [keep.tile([P, HALF], F32, name="cosv%d" % hf) for hf in range(2)]
+        ctab = [[keep.tile([P, HALF], F32, name="ctab%d_%d" % (mat, hf)) for hf in range(2)] for mat in range(2)]
+        stab = [[keep.tile([P, HALF], F32, name="stab%d_%d" % (mat, hf)) for hf in range(2)] for mat in range(2)]
+        red = {}
+
+        def scales(hf):
+            if PATH[hf] == "B":
+                nc.scalar.activation(out=scl[0][hf][:], in_=tok_b[hf][:], func=ACT.Exp, scale=cl[:, 1:2], bias=cl[:, 2:3])
+                nc.scalar.activation(out=scl[1][hf][:], in_=tok_b[hf][:], func=ACT.Exp, scale=cl[:, 3:4], bias=cl[:, 0:1])
+            else:
+                arg = keep.tile([P, HALF], F32, name="arg%d" % hf)
+                for tl in range(4):
+                    t = 4 * hf + tl
+                    nc.gpsimd.tensor_scalar(out=arg[:, tl * P:(tl + 1) * P], in0=kl[:], scalar1=pw_a[:, t:t + 1], scalar2=0.0,
+                                            op0=ALU.mult, op1=ALU.add)
+                nc.scalar.activation(out=scl[0][hf][:], in_=arg[:], func=ACT.Exp)
+                nc.scalar.activation(out=scl[1][hf][:], in_=arg[:], func=ACT.Exp, scale=-1.0)
+
+        def angles_v(hf):
+            t1 = keep.tile([P, HALF], F32, name="t1_%d" % hf)
+            ki = keep.tile([P, HALF], I32, name="ki_%d" % hf)
+            a = keep.tile([P, HALF], F32, name="a_%d" % hf)
+            red[hf] = keep.tile([P, HALF], F32, name="red%d" % hf)
+            if PATH[hf] == "B":
+                nc.vector.tensor_scalar(out=t1[:], in0=tok_b[hf][:], scalar1=cst[:, 2:3], scalar2=MAGIC, op0=ALU.mult, op1=ALU.add)
+                nc.vector.tensor_scalar(out=a[:], in0=tok_b[hf][:], scalar1=cst[:, 0:1], scalar2=None, op0=ALU.mult)
+            else:
+                for tl in range(4):
+                    t = 4 * hf + tl
+                    nc.vector.tensor_scalar(out=a[:, tl * P:(tl + 1) * P], in0=wsgn[:], scalar1=tok_a[:, t:t + 1], scalar2=None,
+                                            op0=ALU.mult)
+                nc.vector.tensor_scalar(out=t1[:], in0=a[:], scalar1=1.0 / TWO_PI, scalar2=MAGIC, op0=ALU.mult, op1=ALU.add)
+            nc.vector.tensor_scalar(out=ki[:], in0=t1[:], scalar1=-MAGIC, scalar2=None, op0=ALU.add)
+            nc.vector.scalar_tensor_tensor(out=red[hf][:], in0=ki[:], scalar=-TWO_PI, in1=a[:], op0=ALU.mult, op1=ALU.add)
+
+        def angles_s(hf):
+            if PATH[hf] == "B":
+                nc.scalar.activation(out=sinv[hf][:], in_=red[hf][:], func=ACT.Sin, scale=cst[:, 1:2])
+            else:
+                nc.scalar.activation(out=sinv[hf][:], in_=red[hf][:], func=ACT.Sin)
+            ab = keep.tile([P, HALF], F32, name="ab%d" % hf)
+            nc.scalar.activation(out=ab[:], in_=red[hf][:], func=ACT.Abs)
+            nc.scalar.activation(out=cosv[hf][:], in_=ab[:], func=ACT.Sin, scale=-1.0, bias=0.5 * math.pi)
+
+        def tables(mat, hf, eng):
+            eng.tensor_tensor(out=ctab[mat][hf][:], in0=cosv[hf][:], in1=scl[mat][hf][:], op=ALU.mult)
+            eng.tensor_tensor(out=stab[mat][hf][:], in0=sinv[hf][:], in1=scl[mat][hf][:], op=ALU.mult)
 
         xg = [[keep.tile([P, HALF, 4], BF16, name="xg%d_%d" % (g, hf), align_bytes=64) for hf in range(2)] for g in range(2)]
         xc = [[keep.tile([P, HALF], U32, name="xc%d_%d" % (g, hf), align_bytes=64) for hf in range(2)] for g in range(2)]
@@ -165,49 +216,10 @@ def tile_gatedmultiscaleretentionlayer_pa_kernel(tc, x, Wq, bq, Wk, bk, out_0, o
                 nc.vector.quantize_mx(out=xc[g][hf][:, c0:c0 + 256].bitcast(FP8X4), scales=xs[g][hf][:, c0:c0 + 256],
                                       in_=xg[g][hf][:, c0:c0 + 256, :].rearrange("p c j -> p (c j)"))
 
-        sinv = keep.tile([P, S], F32, name="sinv")
-        cosv = keep.tile([P, S], F32, name="cosv")
-        ctab = [keep.tile([P, S], F32, name="ctab%d" % mat) for mat in range(2)]
-        stab = [keep.tile([P, S], F32, name="stab%d" % mat) for mat in range(2)]
-        red = {}
-
-        def angles_v(hf):
-            cols = slice(hf * HALF, (hf + 1) * HALF)
-            t1 = tmp.tile([P, HALF], F32, tag="tmp")
-            nc.vector.tensor_scalar(out=t1[:], in0=tokf[:, cols], scalar1=cst[:, 2:3], scalar2=MAGIC, op0=ALU.mult, op1=ALU.add)
-            ki = tmp.tile([P, HALF], I32, tag="tmp")
-            nc.vector.tensor_scalar(out=ki[:], in0=t1[:], scalar1=-MAGIC, scalar2=None, op0=ALU.add)
-            a = tmp.tile([P, HALF], F32, tag="tmp")
-            nc.vector.tensor_scalar(out=a[:], in0=tokf[:, cols], scalar1=cst[:, 0:1], scalar2=None, op0=ALU.mult)
-            red[hf] = tmp.tile([P, HALF], F32, tag="tmp", name="red")
-            nc.vector.scalar_tensor_tensor(out=red[hf][:], in0=ki[:], scalar=-TWO_PI, in1=a[:], op0=ALU.mult, op1=ALU.add)
-
-        def angles_s(hf):
-            cols = slice(hf * HALF, (hf + 1) * HALF)
-            nc.scalar.activation(out=sinv[:, cols], in_=red[hf][:], func=ACT.Sin, scale=cst[:, 1:2])
-            ab = keep.tile([P, HALF], F32, name="ab%d" % hf)
-            nc.scalar.activation(out=ab[:], in_=red[hf][:], func=ACT.Abs)
-            nc.scalar.activation(out=cosv[:, cols], in_=ab[:], func=ACT.Sin, scale=-1.0, bias=0.5 * math.pi)
-
-        def tables_q(hf, eng):
-            cols = slice(hf * HALF, (hf + 1) * HALF)
-            eng.tensor_tensor(out=ctab[0][:, cols], in0=cosv[:, cols], in1=sq[:, cols], op=ALU.mult)
-            eng.tensor_tensor(out=stab[0][:, cols], in0=sinv[:, cols], in1=sq[:, cols], op=ALU.mult)
-
-        def tables_k(step):
-            if step < 2:
-                for t in range(4 * step, 4 * step + 4):
-                    nc.gpsimd.tensor_scalar(out=sk[:, t * P:(t + 1) * P], in0=e2k[:], scalar1=e1k[:, t:t + 1], scalar2=0.0,
-                                            op0=ALU.mult, op1=ALU.add)
-            else:
-                cols = slice((step - 2) * HALF, (step - 1) * HALF)
-                nc.gpsimd.tensor_tensor(out=ctab[1][:, cols], in0=cosv[:, cols], in1=sk[:, cols], op=ALU.mult)
-                nc.gpsimd.tensor_tensor(out=stab[1][:, cols], in0=sinv[:, cols], in1=sk[:, cols], op=ALU.mult)
-
         unit_of = {0: (0, 1), 1: (1, 1)}
-        for a in range(2, NT, 2):
-            unit_of[a] = (a, 2)
-            unit_of[a + 1] = (a, 2)
+        for a0 in range(2, NT, 2):
+            unit_of[a0] = (a0, 2)
+            unit_of[a0 + 1] = (a0, 2)
         g4 = {}
         wc = {}
         ws = {}
@@ -247,31 +259,20 @@ def tile_gatedmultiscaleretentionlayer_pa_kernel(tc, x, Wq, bq, Wk, bk, out_0, o
                                         rhs=xc[g][hf][:].bitcast(FP8X4), rhs_scale=xs[g][hf][:],
                                         start=(g == 0), stop=(g == 1))
 
-        def rot_v(i, hf):
+        def store(i, hf, osb):
+            nc.sync.dma_start(out=outv[i // H][i % H][:, 4 * hf:4 * hf + 4, :], in_=osb[:])
+
+        def rot_b(i, hf):
             mat = i // H
-            cols = slice(hf * HALF, (hf + 1) * HALF)
-            u = uvp.tile([P, HALF], F32, tag="u")
-            v = uvp.tile([P, HALF], F32, tag="v")
-            nc.vector.scalar_tensor_tensor(out=u[:], in0=acc[i][hf][:], scalar=biasT[:, i:i + 1], in1=ctab[mat][:, cols],
+            u = bp.tile([P, HALF], F32, tag="u")
+            v = bp.tile([P, HALF], F32, tag="v")
+            nc.vector.scalar_tensor_tensor(out=u[:], in0=acc[i][hf][:], scalar=biasT[:, i:i + 1], in1=ctab[mat][hf][:],
                                            op0=ALU.add, op1=ALU.mult)
-            nc.vector.scalar_tensor_tensor(out=v[:], in0=acc[i][hf][:], scalar=biasT[:, i:i + 1], in1=stab[mat][:, cols],
+            nc.vector.scalar_tensor_tensor(out=v[:], in0=acc[i][hf][:], scalar=biasT[:, i:i + 1], in1=stab[mat][hf][:],
                                            op0=ALU.add, op1=ALU.mult)
             uv[(i, hf)] = (u, v)
 
-        def rot_s(i, hf):
-            tsb[(i, hf)] = gvp.tile([P, HALF], F32, tag="t", name="tsb")
-            nc.scalar.activation(out=tsb[(i, hf)][:], in_=acc[i][hf][:], func=ACT.Identity, bias=biasT[:, i:i + 1])
-
-        def rot_g(i, hf):
-            mat = i // H
-            cols = slice(hf * HALF, (hf + 1) * HALF)
-            u = gvp.tile([P, HALF], F32, tag="ug")
-            v = gvp.tile([P, HALF], F32, tag="vg")
-            nc.gpsimd.tensor_tensor(out=u[:], in0=tsb[(i, hf)][:], in1=ctab[mat][:, cols], op=ALU.mult)
-            nc.gpsimd.tensor_tensor(out=v[:], in0=tsb[(i, hf)][:], in1=stab[mat][:, cols], op=ALU.mult)
-            uv[(i, hf)] = (u, v)
-
-        def back(i, hf):
+        def back_b(i, hf):
             u, v = uv[(i, hf)]
             o = pstp.tile([P, 4, DK], F32, tag="tp")
             for tl in range(4):
@@ -280,15 +281,40 @@ def tile_gatedmultiscaleretentionlayer_pa_kernel(tc, x, Wq, bq, Wk, bk, out_0, o
                 nc.tensor.matmul(out=o[:, tl, :], lhsT=v[:, blk], rhs=swap[:], is_transpose=True, start=False, stop=True)
             otp[(i, hf)] = o
 
-        def leave(i, hf, eng):
-            mat, h = i // H, i % H
+        def leave_b(i, hf):
             osb = outp.tile([P, 4, DK], F32, tag="o")
-            if eng == "v":
-                nc.vector.tensor_copy(out=osb[:], in_=otp[(i, hf)][:])
-            else:
-                nc.scalar.copy(out=osb[:], in_=otp[(i, hf)][:])
-            nc.sync.dma_start(out=outv[mat][h][:, 4 * hf:4 * hf + 4, :], in_=osb[:])
+            nc.scalar.copy(out=osb[:], in_=otp[(i, hf)][:])
+            store(i, hf, osb)
 
+        def evac_a(i, hf):
+            tsb[(i, hf)] = ap.tile([P, HALF], F32, tag="t", name="tsb")
+            nc.scalar.activation(out=tsb[(i, hf)][:], in_=acc[i][hf][:], func=ACT.Identity, bias=biasT[:, i:i + 1])
+
+        def back_a(i, hf):
+            o = pstp.tile([P, 4, DK], F32, tag="tp")
+            for tl in range(4):
+                nc.tensor.transpose(o[:, tl, :], tsb[(i, hf)][:, tl * P:(tl + 1) * P], ident[:])
+            otp[(i, hf)] = o
+
+        def rot_a(i, hf):
+            mat = i // H
+            o = otp[(i, hf)]
+            u = ap.tile([P, HALF], F32, tag="ua")
+            v = ap.tile([P, HALF], F32, tag="va")
+            nc.vector.tensor_tensor(out=u[:], in0=o[:].rearrange("p t f -> p (t f)"), in1=ctab[mat][hf][:], op=ALU.mult)
+            nc.vector.tensor_tensor(out=v[:].rearrange("p (n e) -> p n e", e=2),
+                                    in0=o[:].rearrange("p t (m e) -> p (t m) e", e=2)[:, :, ::-1],
+                                    in1=stab[mat][hf][:].rearrange("p (n e) -> p n e", e=2), op=ALU.mult)
+            uv[(i, hf)] = (u, v)
+
+        def add_a(i, hf):
+            u, v = uv[(i, hf)]
+            osb = outp.tile([P, 4, DK], F32, tag="o")
+            nc.gpsimd.tensor_tensor(out=osb[:].rearrange("p t f -> p (t f)"), in0=u[:], in1=v[:], op=ALU.add)
+            store(i, hf, osb)
+
+        scales(0)
+        scales(1)
         angles_v(0)
         angles_s(0)
         angles_v(1)
@@ -305,8 +331,8 @@ def tile_gatedmultiscaleretentionlayer_pa_kernel(tc, x, Wq, bq, Wk, bk, out_0, o
         nc.vector.tensor_copy(out=biasT[:], in_=bt_ps[:, 0:2 * H])
         x_pair(2, "ss")
         x_pair(3, "ss")
-        tables_q(0, nc.vector)
-        tables_q(1, nc.gpsimd)
+        tables(0, 0, nc.vector)
+        tables(0, 1, nc.gpsimd)
         inter(1, "s")
         x_quant(2)
         x_quant(3)
@@ -314,31 +340,31 @@ def tile_gatedmultiscaleretentionlayer_pa_kernel(tc, x, Wq, bq, Wk, bk, out_0, o
         inter(2, "g")
         inter(3, "g")
 
-        NP = NT // 2
-        for p in range(NP + 1):
-            if p + 1 < NP:
-                quant(2 * p + 2)
-            if p < NP:
-                mx(2 * p)
-                mx(2 * p + 1)
-                if 2 * p + 5 < NT:
-                    inter(2 * p + 4, "s")
-                    inter(2 * p + 5, "g")
-                banks = [(2 * p, 0), (2 * p, 1), (2 * p + 1, 0), (2 * p + 1, 1)]
-                for b in banks:
-                    if not g_rot(b[0], b[1]):
-                        rot_v(b[0], b[1])
-                for b in banks:
-                    if g_rot(b[0], b[1]):
-                        rot_s(b[0], b[1])
-                        rot_g(b[0], b[1])
-            if p > 0:
-                banks = [(2 * p - 2, 0), (2 * p - 2, 1), (2 * p - 1, 0), (2 * p - 1, 1)]
-                for b in banks:
-                    back(b[0], b[1])
-                for n, b in enumerate(banks):
-                    leave(b[0], b[1], "v" if (p == NP and n % 2 == 0) else "s")
-            if p % 2 == 1 and 3 <= (p + 5) // 2 < 8:
-                load_w((p + 5) // 2, 0, HALF)
-            if 2 <= p < 6:
-                tables_k(p - 2)
+        def tiles_at(t, kind):
+            return [(t, hf) for hf in range(2) if 0 <= t < NT and PATH[hf] == kind]
+
+        for s in range(NT + 5):
+            if s < NT:
+                mx(s)
+            for b in tiles_at(s - 1, "A"):
+                evac_a(b[0], b[1])
+            for b in tiles_at(s - 1, "B"):
+                rot_b(b[0], b[1])
+            for b in tiles_at(s - 3, "A"):
+                rot_a(b[0], b[1])
+            for b in tiles_at(s - 3, "B"):
+                leave_b(b[0], b[1])
+            for b in tiles_at(s - 4, "A"):
+                add_a(b[0], b[1])
+            if s % 2 == 0 and s + 2 < NT:
+                quant(s + 2)
+            for b in tiles_at(s - 2, "B"):
+                back_b(b[0], b[1])
+            for b in tiles_at(s - 2, "A"):
+                back_a(b[0], b[1])
+            if s + 4 < NT:
+                inter(s + 4, inter_engine(s + 4))
+            if s % 4 == 2 and 3 <= (s + 10) // 4 < 8:
+                load_w((s + 10) // 4, 0, HALF)
+            if s == 4 or s == 6:
+                tables(1, (s - 4) // 2, nc.gpsimd)

@@ -30,8 +30,12 @@ NB = PATH.count("B")
 NA = PATH.count("A")
 
 
+def g_rot(i):
+    return i % 4 == 1 and i < 28
+
+
 def inter_engine(i):
-    return "g" if i % 2 == 1 else "s"
+    return "s"
 
 
 def tile_gatedmultiscaleretentionlayer_pa_kernel(tc, x, Wq, bq, Wk, bk, out_0, out_1):
@@ -42,8 +46,9 @@ def tile_gatedmultiscaleretentionlayer_pa_kernel(tc, x, Wq, bq, Wk, bk, out_0, o
         wrp = ctx.enter_context(tc.tile_pool(name="wrp", bufs=4))
         grp = ctx.enter_context(tc.tile_pool(name="grp", bufs=3))
         wcp = ctx.enter_context(tc.tile_pool(name="wcp", bufs=3))
-        bp = ctx.enter_context(tc.tile_pool(name="bp", bufs=max(3 * NB, 1)))
-        ap = ctx.enter_context(tc.tile_pool(name="ap", bufs=max(3 * NA, 1)))
+        bp = ctx.enter_context(tc.tile_pool(name="bp", bufs=3))
+        gp = ctx.enter_context(tc.tile_pool(name="gp", bufs=2))
+        ap = ctx.enter_context(tc.tile_pool(name="ap", bufs=4))
         outp = ctx.enter_context(tc.tile_pool(name="outp", bufs=8))
         psmx = ctx.enter_context(tc.psum_pool(name="psmx", bufs=4))
         pstp = ctx.enter_context(tc.psum_pool(name="pstp", bufs=4))
@@ -272,6 +277,14 @@ def tile_gatedmultiscaleretentionlayer_pa_kernel(tc, x, Wq, bq, Wk, bk, out_0, o
                                            op0=ALU.add, op1=ALU.mult)
             uv[(i, hf)] = (u, v)
 
+        def rot_g(i, hf):
+            mat = i // H
+            u = gp.tile([P, HALF], F32, tag="ug")
+            v = gp.tile([P, HALF], F32, tag="vg")
+            nc.gpsimd.tensor_tensor(out=u[:], in0=tsb[(i, hf)][:], in1=ctab[mat][hf][:], op=ALU.mult)
+            nc.gpsimd.tensor_tensor(out=v[:], in0=tsb[(i, hf)][:], in1=stab[mat][hf][:], op=ALU.mult)
+            uv[(i, hf)] = (u, v)
+
         def back_b(i, hf):
             u, v = uv[(i, hf)]
             o = pstp.tile([P, 4, DK], F32, tag="tp")
@@ -310,7 +323,8 @@ def tile_gatedmultiscaleretentionlayer_pa_kernel(tc, x, Wq, bq, Wk, bk, out_0, o
         def add_a(i, hf):
             u, v = uv[(i, hf)]
             osb = outp.tile([P, 4, DK], F32, tag="o")
-            nc.gpsimd.tensor_tensor(out=osb[:].rearrange("p t f -> p (t f)"), in0=u[:], in1=v[:], op=ALU.add)
+            eng = nc.vector if i >= 31 else nc.gpsimd
+            eng.tensor_tensor(out=osb[:].rearrange("p t f -> p (t f)"), in0=u[:], in1=v[:], op=ALU.add)
             store(i, hf, osb)
 
         scales(0)
@@ -337,28 +351,36 @@ def tile_gatedmultiscaleretentionlayer_pa_kernel(tc, x, Wq, bq, Wk, bk, out_0, o
         x_quant(2)
         x_quant(3)
         quant(1)
-        inter(2, "g")
-        inter(3, "g")
+        inter(2, "v")
+        inter(3, "v")
 
         def tiles_at(t, kind):
-            return [(t, hf) for hf in range(2) if 0 <= t < NT and PATH[hf] == kind]
+            if not 0 <= t < NT:
+                return []
+            if kind == "A":
+                return [(t, 1)]
+            if (kind == "G") == g_rot(t):
+                return [(t, 0)]
+            return []
 
-        for s in range(NT + 5):
+        for s in range(NT + 6):
             if s < NT:
                 mx(s)
-            for b in tiles_at(s - 1, "A"):
+            for b in tiles_at(s - 1, "A") + tiles_at(s - 1, "G"):
                 evac_a(b[0], b[1])
             for b in tiles_at(s - 1, "B"):
                 rot_b(b[0], b[1])
             for b in tiles_at(s - 3, "A"):
                 rot_a(b[0], b[1])
-            for b in tiles_at(s - 3, "B"):
+            for b in tiles_at(s - 3, "B") + tiles_at(s - 5, "G"):
                 leave_b(b[0], b[1])
             for b in tiles_at(s - 4, "A"):
                 add_a(b[0], b[1])
+            for b in tiles_at(s - 2, "G"):
+                rot_g(b[0], b[1])
             if s % 2 == 0 and s + 2 < NT:
                 quant(s + 2)
-            for b in tiles_at(s - 2, "B"):
+            for b in tiles_at(s - 2, "B") + tiles_at(s - 4, "G"):
                 back_b(b[0], b[1])
             for b in tiles_at(s - 2, "A"):
                 back_a(b[0], b[1])

@@ -124,7 +124,7 @@ def tile_gatedmultiscaleretentionlayer_pa_kernel(tc, x, Wq, bq, Wk, bk, out_0, o
         wsgn = keep.tile([P, P], F32, name="wsgn")
         pw_a = keep.tile([P, TB], F32, name="pw_a")
         if NA > 0:
-            nc.vector.scalar_tensor_tensor(out=wsgn[:], in0=kc[:, 0, :], scalar=-1.0, in1=kc[:, 1, :], op0=ALU.mult, op1=ALU.mult)
+            nc.vector.tensor_tensor(out=wsgn[:], in0=kc[:, 0, :], in1=kc[:, 1, :], op=ALU.mult)
             nc.vector.tensor_scalar(out=pw_a[:], in0=tok_a[:], scalar1=-512.0, scalar2=1.0 / 512.0, op0=ALU.add, op1=ALU.mult)
         if NB > 0:
             kta = pstp.tile([P, 2, P], F32, tag="tp")
@@ -144,10 +144,11 @@ def tile_gatedmultiscaleretentionlayer_pa_kernel(tc, x, Wq, bq, Wk, bk, out_0, o
             nc.vector.tensor_scalar(out=cl[:, 3:4], in0=cl[:, 0:1], scalar1=-1.0 / 512.0, scalar2=None, op0=ALU.mult)
 
         scl = [[keep.tile([P, HALF], F32, name="scl%d_%d" % (mat, hf)) for hf in range(2)] for mat in range(2)]
-        sinv = [keep.tile([P, HALF], F32, name="sinv%d" % hf) for hf in range(2)]
-        cosv = [keep.tile([P, HALF], F32, name="cosv%d" % hf) for hf in range(2)]
-        ctab = [[keep.tile([P, HALF], F32, name="ctab%d_%d" % (mat, hf)) for hf in range(2)] for mat in range(2)]
-        stab = [[keep.tile([P, HALF], F32, name="stab%d_%d" % (mat, hf)) for hf in range(2)] for mat in range(2)]
+        trig = [keep.tile([P, 2, HALF], F32, name="trig%d" % hf) for hf in range(2)]
+        cs = [[keep.tile([P, 2, HALF], F32, name="cs%d_%d" % (mat, hf)) for hf in range(2)] for mat in range(2)]
+
+        def twice(ap):
+            return ap.unsqueeze(1).to_broadcast([P, 2, HALF])
         red = {}
 
         def scales(hf):
@@ -182,16 +183,15 @@ def tile_gatedmultiscaleretentionlayer_pa_kernel(tc, x, Wq, bq, Wk, bk, out_0, o
 
         def angles_s(hf):
             if PATH[hf] == "B":
-                nc.scalar.activation(out=sinv[hf][:], in_=red[hf][:], func=ACT.Sin, scale=cst[:, 1:2])
+                nc.scalar.activation(out=trig[hf][:, 1, :], in_=red[hf][:], func=ACT.Sin, scale=cst[:, 1:2])
             else:
-                nc.scalar.activation(out=sinv[hf][:], in_=red[hf][:], func=ACT.Sin)
+                nc.scalar.activation(out=trig[hf][:, 1, :], in_=red[hf][:], func=ACT.Sin)
             ab = keep.tile([P, HALF], F32, name="ab%d" % hf)
             nc.scalar.activation(out=ab[:], in_=red[hf][:], func=ACT.Abs)
-            nc.scalar.activation(out=cosv[hf][:], in_=ab[:], func=ACT.Sin, scale=-1.0, bias=0.5 * math.pi)
+            nc.scalar.activation(out=trig[hf][:, 0, :], in_=ab[:], func=ACT.Sin, scale=-1.0, bias=0.5 * math.pi)
 
         def tables(mat, hf, eng):
-            eng.tensor_tensor(out=ctab[mat][hf][:], in0=cosv[hf][:], in1=scl[mat][hf][:], op=ALU.mult)
-            eng.tensor_tensor(out=stab[mat][hf][:], in0=sinv[hf][:], in1=scl[mat][hf][:], op=ALU.mult)
+            eng.tensor_tensor(out=cs[mat][hf][:], in0=trig[hf][:], in1=twice(scl[mat][hf][:]), op=ALU.mult)
 
         xg = [[keep.tile([P, HALF, 4], BF16, name="xg%d_%d" % (g, hf), align_bytes=64) for hf in range(2)] for g in range(2)]
         xc = [[keep.tile([P, HALF], U32, name="xc%d_%d" % (g, hf), align_bytes=64) for hf in range(2)] for g in range(2)]
@@ -269,29 +269,24 @@ def tile_gatedmultiscaleretentionlayer_pa_kernel(tc, x, Wq, bq, Wk, bk, out_0, o
 
         def rot_b(i, hf):
             mat = i // H
-            u = bp.tile([P, HALF], F32, tag="u")
-            v = bp.tile([P, HALF], F32, tag="v")
-            nc.vector.scalar_tensor_tensor(out=u[:], in0=acc[i][hf][:], scalar=biasT[:, i:i + 1], in1=ctab[mat][hf][:],
+            w = bp.tile([P, 2, HALF], F32, tag="uv")
+            nc.vector.scalar_tensor_tensor(out=w[:], in0=twice(acc[i][hf][:]), scalar=biasT[:, i:i + 1], in1=cs[mat][hf][:],
                                            op0=ALU.add, op1=ALU.mult)
-            nc.vector.scalar_tensor_tensor(out=v[:], in0=acc[i][hf][:], scalar=biasT[:, i:i + 1], in1=stab[mat][hf][:],
-                                           op0=ALU.add, op1=ALU.mult)
-            uv[(i, hf)] = (u, v)
+            uv[(i, hf)] = w
 
         def rot_g(i, hf):
             mat = i // H
-            u = gp.tile([P, HALF], F32, tag="ug")
-            v = gp.tile([P, HALF], F32, tag="vg")
-            nc.gpsimd.tensor_tensor(out=u[:], in0=tsb[(i, hf)][:], in1=ctab[mat][hf][:], op=ALU.mult)
-            nc.gpsimd.tensor_tensor(out=v[:], in0=tsb[(i, hf)][:], in1=stab[mat][hf][:], op=ALU.mult)
-            uv[(i, hf)] = (u, v)
+            w = gp.tile([P, 2, HALF], F32, tag="uvg")
+            nc.gpsimd.tensor_tensor(out=w[:], in0=twice(tsb[(i, hf)][:]), in1=cs[mat][hf][:], op=ALU.mult)
+            uv[(i, hf)] = w
 
         def back_b(i, hf):
-            u, v = uv[(i, hf)]
+            w = uv[(i, hf)]
             o = pstp.tile([P, 4, DK], F32, tag="tp")
             for tl in range(4):
                 blk = slice(tl * P, (tl + 1) * P)
-                nc.tensor.matmul(out=o[:, tl, :], lhsT=u[:, blk], rhs=ident[:], is_transpose=True, start=True, stop=False)
-                nc.tensor.matmul(out=o[:, tl, :], lhsT=v[:, blk], rhs=swap[:], is_transpose=True, start=False, stop=True)
+                nc.tensor.matmul(out=o[:, tl, :], lhsT=w[:, 0, blk], rhs=ident[:], is_transpose=True, start=True, stop=False)
+                nc.tensor.matmul(out=o[:, tl, :], lhsT=w[:, 1, blk], rhs=swap[:], is_transpose=True, start=False, stop=True)
             otp[(i, hf)] = o
 
         def leave_b(i, hf):
@@ -312,19 +307,17 @@ def tile_gatedmultiscaleretentionlayer_pa_kernel(tc, x, Wq, bq, Wk, bk, out_0, o
         def rot_a(i, hf):
             mat = i // H
             o = otp[(i, hf)]
-            u = ap.tile([P, HALF], F32, tag="ua")
-            v = ap.tile([P, HALF], F32, tag="va")
-            nc.vector.tensor_tensor(out=u[:], in0=o[:].rearrange("p t f -> p (t f)"), in1=ctab[mat][hf][:], op=ALU.mult)
-            nc.vector.tensor_tensor(out=v[:].rearrange("p (n e) -> p n e", e=2),
-                                    in0=o[:].rearrange("p t (m e) -> p (t m) e", e=2)[:, :, ::-1],
-                                    in1=stab[mat][hf][:].rearrange("p (n e) -> p n e", e=2), op=ALU.mult)
-            uv[(i, hf)] = (u, v)
+            w = ap.tile([P, 2, HALF], F32, tag="uva")
+            nc.vector.tensor_tensor(out=w[:], in0=twice(o[:].rearrange("p t f -> p (t f)")), in1=cs[mat][hf][:], op=ALU.mult)
+            uv[(i, hf)] = w
 
         def add_a(i, hf):
-            u, v = uv[(i, hf)]
+            w = uv[(i, hf)]
             osb = outp.tile([P, 4, DK], F32, tag="o")
             eng = nc.vector if i >= 31 else nc.gpsimd
-            eng.tensor_tensor(out=osb[:].rearrange("p t f -> p (t f)"), in0=u[:], in1=v[:], op=ALU.add)
+            eng.tensor_tensor(out=osb[:].rearrange("p t (m e) -> p (t m) e", e=2),
+                              in0=w[:, 0, :].rearrange("p (n e) -> p n e", e=2),
+                              in1=w[:, 1, :].rearrange("p (n e) -> p n e", e=2)[:, :, ::-1], op=ALU.add)
             store(i, hf, osb)
 
         scales(0)

@@ -238,8 +238,8 @@ def tile_gatedmultiscaleretentionlayer_pa_kernel(tc, x, Wq, bq, Wk, bk, out_0, o
             if i == a:
                 g4[a] = grp.tile([P, 2, n * DK, 4], BF16, tag="grp", name="g4", align_bytes=64)
             c0 = (i % 4) * DK
-            src = wraw[i // 4][:, :, :, c0:c0 + DK].rearrange("p g j c -> p g c j")
-            dst = g4[a][:, :, (i - a) * DK:(i - a + 1) * DK, :]
+            src = wraw[i // 4][:, :, :, c0:c0 + DK].rearrange("p g j (c q) -> p g c j q", q=4)
+            dst = g4[a][:, :, (i - a) * DK:(i - a + 1) * DK, :].rearrange("p g (c q) j -> p g c j q", q=4)
             if eng == "v":
                 nc.vector.tensor_copy(out=dst, in_=src)
             elif eng == "g":

@@ -256,7 +256,7 @@ def tile_gatedmultiscaleretentionlayer_pa_kernel(tc, x, Wq, bq, Wk, bk, out_0, o
         def mx(i):
             a, n = unit_of[i]
             acc[i] = [psmx.tile([P, HALF], F32, tag="mx", name="acc%d" % hf) for hf in range(2)]
-            for hf in range(2):
+            for hf in (1, 0):
                 for g in range(2):
                     c0 = (g * n + i - a) * DK
                     nc.tensor.matmul_mx(out=acc[i][hf][:],
@@ -373,10 +373,10 @@ def tile_gatedmultiscaleretentionlayer_pa_kernel(tc, x, Wq, bq, Wk, bk, out_0, o
                 rot_g(b[0], b[1])
             if s % 2 == 0 and s + 2 < NT:
                 quant(s + 2)
-            for b in tiles_at(s - 2, "B") + tiles_at(s - 4, "G"):
-                back_b(b[0], b[1])
             for b in tiles_at(s - 2, "A"):
                 back_a(b[0], b[1])
+            for b in tiles_at(s - 2, "B") + tiles_at(s - 4, "G"):
+                back_b(b[0], b[1])
             if s + 4 < NT:
                 inter(s + 4, inter_engine(s + 4))
             if s % 4 == 2 and 3 <= (s + 10) // 4 < 8:

@@ -159,8 +159,8 @@ def tile_gatedmultiscaleretentionlayer_pa_kernel(tc, x, Wq, bq, Wk, bk, out_0, o
                 arg = keep.tile([P, HALF], F32, name="arg%d" % hf)
                 for tl in range(4):
                     t = 4 * hf + tl
-                    nc.gpsimd.tensor_scalar(out=arg[:, tl * P:(tl + 1) * P], in0=kl[:], scalar1=pw_a[:, t:t + 1], scalar2=0.0,
-                                            op0=ALU.mult, op1=ALU.add)
+                    nc.vector.tensor_scalar(out=arg[:, tl * P:(tl + 1) * P], in0=kl[:], scalar1=pw_a[:, t:t + 1], scalar2=None,
+                                            op0=ALU.mult)
                 nc.scalar.activation(out=scl[0][hf][:], in_=arg[:], func=ACT.Exp)
                 nc.scalar.activation(out=scl[1][hf][:], in_=arg[:], func=ACT.Exp, scale=-1.0)
 
@@ -339,7 +339,7 @@ def tile_gatedmultiscaleretentionlayer_pa_kernel(tc, x, Wq, bq, Wk, bk, out_0, o
         x_pair(2, "ss")
         x_pair(3, "ss")
         tables(0, 0, nc.vector)
-        tables(0, 1, nc.gpsimd)
+        tables(0, 1, nc.vector)
         inter(1, "s")
         x_quant(2)
         x_quant(3)

@@ -59,8 +59,17 @@ def tile_gatedmultiscaleretentionlayer_pa_kernel(tc, x, Wq, bq, Wk, bk, out_0, o
 
         x_sb = [keep.tile([P, 2, D], BF16, name="x_sb%d" % tp) for tp in range(4)]
         wraw = {}
+        zt = keep.tile([P, HALF], BF16, name="zt")
+        nc.vector.memset(zt[:], 0.0)
         btile = keep.tile([P, P], BF16, name="btile")
         nc.vector.memset(btile[:], 0.0)
+
+        def keep_warm(n):
+            dps = psmx.tile([P, HALF], F32, tag="mx", name="dps")
+            for r in range(n):
+                nc.tensor.matmul(out=dps[:], lhsT=zt[:, 0:P], rhs=zt[:], start=True, stop=True)
+
+        keep_warm(5)
 
         def load_x(tp):
             nc.sync.dma_start(out=x_sb[tp][:], in_=xv[:, 2 * tp:2 * tp + 2, :])
@@ -326,8 +335,10 @@ def tile_gatedmultiscaleretentionlayer_pa_kernel(tc, x, Wq, bq, Wk, bk, out_0, o
         angles_s(0)
         angles_v(1)
         x_pair(0, "vv")
+        keep_warm(2)
         x_quant(0)
         x_pair(1, "vv")
+        keep_warm(2)
         x_quant(1)
         angles_s(1)
         inter(0, "v")
@@ -337,6 +348,7 @@ def tile_gatedmultiscaleretentionlayer_pa_kernel(tc, x, Wq, bq, Wk, bk, out_0, o
         biasT = keep.tile([P, 2 * H], F32, name="biasT")
         nc.vector.tensor_copy(out=biasT[:], in_=bt_ps[:, 0:2 * H])
         x_pair(2, "ss")
+        keep_warm(2)
         x_pair(3, "ss")
         tables(0, 0, nc.vector)
         tables(0, 1, nc.vector)

@@ -25,17 +25,18 @@ HALF = 512
 TWO_PI = 2.0 * math.pi
 MAGIC = 12582912.0
 NT = 2 * H
-PATH = ("B", "A")
-NB = PATH.count("B")
-NA = PATH.count("A")
+INTER_G = ()
+GM = 4
+HEAD_ENG = "v"
+ENG45 = "v"
 
 
 def g_rot(i):
-    return i % 4 == 1 and i < 28
+    return i % GM == 1 and i < 30
 
 
 def inter_engine(i):
-    return "s"
+    return "g" if i in INTER_G else "s"
 
 
 def tile_gatedmultiscaleretentionlayer_pa_kernel(tc, x, Wq, bq, Wk, bk, out_0, out_1):
@@ -43,11 +44,12 @@ def tile_gatedmultiscaleretentionlayer_pa_kernel(tc, x, Wq, bq, Wk, bk, out_0, o
     with ExitStack() as ctx:
         ctx.enter_context(tc.manual_schedule())
         keep = ctx.enter_context(tc.tile_pool(name="keep", bufs=1))
-        wrp = ctx.enter_context(tc.tile_pool(name="wrp", bufs=4))
-        grp = ctx.enter_context(tc.tile_pool(name="grp", bufs=3))
-        wcp = ctx.enter_context(tc.tile_pool(name="wcp", bufs=3))
+        wrp = ctx.enter_context(tc.tile_pool(name="wrp", bufs=8))
+        grp = ctx.enter_context(tc.tile_pool(name="grp", bufs=4))
+        wcp = ctx.enter_context(tc.tile_pool(name="wcp", bufs=4))
         bp = ctx.enter_context(tc.tile_pool(name="bp", bufs=3))
         gp = ctx.enter_context(tc.tile_pool(name="gp", bufs=2))
+        dp = ctx.enter_context(tc.tile_pool(name="dp", bufs=2))
         ap = ctx.enter_context(tc.tile_pool(name="ap", bufs=4))
         outp = ctx.enter_context(tc.tile_pool(name="outp", bufs=8))
         psmx = ctx.enter_context(tc.psum_pool(name="psmx", bufs=4))
@@ -60,9 +62,9 @@ def tile_gatedmultiscaleretentionlayer_pa_kernel(tc, x, Wq, bq, Wk, bk, out_0, o
         x_sb = [keep.tile([P, 2, D], BF16, name="x_sb%d" % tp) for tp in range(4)]
         wraw = {}
         zt = keep.tile([P, HALF], BF16, name="zt")
-        nc.vector.memset(zt[:], 0.0)
         btile = keep.tile([P, P], BF16, name="btile")
         nc.vector.memset(btile[:], 0.0)
+        nc.vector.memset(zt[:], 0.0)
 
         def keep_warm(n):
             dps = psmx.tile([P, HALF], F32, tag="mx", name="dps")
@@ -85,122 +87,135 @@ def tile_gatedmultiscaleretentionlayer_pa_kernel(tc, x, Wq, bq, Wk, bk, out_0, o
         load_w(0, 0, 256)
         load_x(2)
         load_x(3)
-        nc.sync.dma_start(out=btile[0:H, :], in_=bq.rearrange("(h c) -> h c", c=DK))
-        nc.sync.dma_start(out=btile[H:2 * H, :], in_=bk.rearrange("(h c) -> h c", c=DK))
         load_w(0, 256, HALF)
         load_w(1, 0, HALF)
         load_w(2, 0, HALF)
 
-        m2 = keep.tile([P, P], F32, name="m2")
-        nc.gpsimd.iota(m2[:], pattern=[[2, 64], [0, 2]], base=0, channel_multiplier=0,
-                       allow_small_or_imprecise_dtypes=True)
+        nc.scalar.dma_start(out=btile[0:H, :], in_=bq.rearrange("(h c) -> h c", c=DK))
+        nc.scalar.dma_start(out=btile[H:2 * H, :], in_=bk.rearrange("(h c) -> h c", c=DK))
+        warm = keep.tile([P, 1], F32, name="warm")
+        nc.scalar.activation(out=warm[:], in_=zt[:, 0:1], func=ACT.Sin)
+
+        pidx = keep.tile([P, 1], I32, name="pidx")
+        nc.gpsimd.iota(pidx[:], pattern=[[0, 1]], base=0, channel_multiplier=1)
         ident = keep.tile([P, P], F32, name="ident")
         make_identity(nc, ident[:])
-        tok_b = {}
-        for hf in range(2):
-            if PATH[hf] == "B":
-                tok_b[hf] = keep.tile([P, HALF], F32, name="tok_b%d" % hf)
-                nc.gpsimd.iota(tok_b[hf][:], pattern=[[1, 4], [TB, P]], base=4 * hf, channel_multiplier=0,
-                               allow_small_or_imprecise_dtypes=True)
-        tok_a = keep.tile([P, TB], F32, name="tok_a")
-        nc.gpsimd.iota(tok_a[:], pattern=[[1, TB]], base=0, channel_multiplier=TB, allow_small_or_imprecise_dtypes=True)
+        NR = P + 3
+        tokr = keep.tile([P, NR], F32, name="tokr")
+        nc.gpsimd.iota(tokr[:, 0:P], pattern=[[TB, P]], base=0, channel_multiplier=0, allow_small_or_imprecise_dtypes=True)
+
+        col_i = keep.tile([P, 2], I32, name="col_i")
+        col = keep.tile([P, 2], F32, name="col")
+        nc.vector.tensor_single_scalar(out=col_i[:, 0:1], in_=pidx[:], scalar=-2, op=ALU.bitwise_and)
+        nc.vector.tensor_single_scalar(out=col_i[:, 1:2], in_=pidx[:], scalar=1, op=ALU.bitwise_and)
+        nc.vector.tensor_copy(out=col[:], in_=col_i[:])
+        NE = 11
+        pb = keep.tile([P, NE], F32, name="pb")
+        pe = keep.tile([P, NE], F32, name="pe")
+        pw = keep.tile([P, NE], F32, name="pw")
+        nc.vector.memset(pb[:, 0:1], 10000.0)
+        nc.vector.tensor_scalar(out=pe[:, 0:1], in0=col[:, 0:1], scalar1=-1.0 / DK, scalar2=None, op0=ALU.mult)
+        nc.gpsimd.tensor_tensor(out=pw[:, 0:1], in0=pb[:, 0:1], in1=pe[:, 0:1], op=ALU.pow)
+        nc.vector.tensor_scalar(out=pb[:, 1:NE], in0=col[:, 0:1].to_broadcast([P, NE - 1]), scalar1=1.0 / (1.4 * DK),
+                                scalar2=0.4 / 1.4, op0=ALU.mult, op1=ALU.add)
+        for j in range(7):
+            nc.vector.memset(pe[:, 1 + j:2 + j], float(1 << j) / 64.0)
+        for j in range(3):
+            nc.vector.memset(pe[:, 8 + j:9 + j], float(1 << j) / 512.0)
+            nc.vector.memset(tokr[:, P + j:P + j + 1], float(1 << j))
+        nc.gpsimd.tensor_tensor(out=pw[:, 1:NE], in0=pb[:, 1:NE], in1=pe[:, 1:NE], op=ALU.pow)
         ident_bf = keep.tile([P, P], BF16, name="ident_bf")
         make_identity(nc, ident_bf[:])
-
-        kl = keep.tile([P, P], F32, name="kl")
-        nc.scalar.activation(out=kl[:], in_=m2[:], func=ACT.Ln, scale=1.0 / (1.4 * DK), bias=(0.4 * DK) / (1.4 * DK))
-
-        ones = keep.tile([P, 16], F32, name="ones")
-        nc.vector.memset(ones[:], 1.0)
-        khi = keep.tile([P, P], F32, name="khi")
-        klo = keep.tile([P, P], F32, name="klo")
-        kc = keep.tile([P, 2, P], F32, name="kc")
-        sgv = kc[:, 1, :].rearrange("p (m e) -> p m e", e=2)
-        nc.vector.memset(sgv[:, :, 0:1], 1.0)
-        nc.vector.memset(sgv[:, :, 1:2], -1.0)
-        klov = klo[:].rearrange("p (h l e) -> p h l e", l=8, e=2)
-        onesv = ones[:].rearrange("p (h e) -> p h e", e=2)
-        for i in range(8):
-            nc.vector.tensor_scalar(out=khi[:, 16 * i:16 * i + 16], in0=ones[:], scalar1=10000.0 ** (-8.0 * i / 64.0),
-                                    scalar2=None, op0=ALU.mult)
-            nc.vector.tensor_scalar(out=klov[:, :, i, :], in0=onesv, scalar1=10000.0 ** (-1.0 * i / 64.0),
-                                    scalar2=None, op0=ALU.mult)
-        nc.vector.tensor_tensor(out=kc[:, 0, :], in0=khi[:], in1=klo[:], op=ALU.mult)
-
-        cst = keep.tile([P, 4], F32, name="cst")
-        cl = keep.tile([P, 4], F32, name="cl")
+        cst = keep.tile([P, 2], F32, name="cst")
+        nc.vector.tensor_scalar(out=cst[:, 1:2], in0=col[:, 1:2], scalar1=-2.0, scalar2=1.0, op0=ALU.mult, op1=ALU.add)
         swap = keep.tile([P, P], F32, name="swap")
-        wsgn = keep.tile([P, P], F32, name="wsgn")
-        pw_a = keep.tile([P, TB], F32, name="pw_a")
-        if NA > 0:
-            nc.vector.tensor_tensor(out=wsgn[:], in0=kc[:, 0, :], in1=kc[:, 1, :], op=ALU.mult)
-            nc.vector.tensor_scalar(out=pw_a[:], in0=tok_a[:], scalar1=-512.0, scalar2=1.0 / 512.0, op0=ALU.add, op1=ALU.mult)
-        if NB > 0:
-            kta = pstp.tile([P, 2, P], F32, tag="tp")
-            for s in range(2):
-                nc.tensor.transpose(kta[:, s, :], kc[:, s, :], ident[:])
-            ktb = pstp.tile([P, P], F32, tag="tp")
-            nc.tensor.transpose(ktb[:], kl[:], ident[:])
-            idv = ident[:].rearrange("p (m e) -> p m e", e=2)
-            swv = swap[:].rearrange("p (m e) -> p m e", e=2)
-            nc.vector.tensor_copy(out=swv[:, :, 0:1], in_=idv[:, :, 1:2])
-            nc.vector.tensor_copy(out=swv[:, :, 1:2], in_=idv[:, :, 0:1])
-            nc.vector.tensor_copy(out=cst[:, 0:2], in_=kta[:].rearrange("p s c -> p c s")[:, 0, :])
-            nc.vector.tensor_scalar(out=cst[:, 2:3], in0=cst[:, 0:1], scalar1=1.0 / TWO_PI, scalar2=None, op0=ALU.mult)
-            nc.vector.tensor_copy(out=cl[:, 0:1], in_=ktb[:, 0:1])
-            nc.vector.tensor_scalar(out=cl[:, 1:2], in0=cl[:, 0:1], scalar1=1.0 / 512.0, scalar2=None, op0=ALU.mult)
-            nc.vector.tensor_scalar(out=cl[:, 2:3], in0=cl[:, 0:1], scalar1=-1.0, scalar2=None, op0=ALU.mult)
-            nc.vector.tensor_scalar(out=cl[:, 3:4], in0=cl[:, 0:1], scalar1=-1.0 / 512.0, scalar2=None, op0=ALU.mult)
 
-        scl = [[keep.tile([P, HALF], F32, name="scl%d_%d" % (mat, hf)) for hf in range(2)] for mat in range(2)]
-        trig = [keep.tile([P, 2, HALF], F32, name="trig%d" % hf) for hf in range(2)]
-        cs = [[keep.tile([P, 2, HALF], F32, name="cs%d_%d" % (mat, hf)) for hf in range(2)] for mat in range(2)]
+        sblk = keep.tile([P, P], F32, name="sblk")
+        trig = keep.tile([P, 2, NR], F32, name="trig")
+        cs = [keep.tile([P, 2, S - HALF * mat], F32, name="cs%d" % mat) for mat in range(2)]
+        rat = keep.tile([P, S], F32, name="rat")
+        pinv = keep.tile([P, NE], F32, name="pinv")
+        pinv2 = keep.tile([P, NE], F32, name="pinv2")
+        dco = keep.tile([P, 2, 3], F32, name="dco")
+        dne = keep.tile([P, 3], F32, name="dne")
+        t1 = keep.tile([P, NR], F32, name="t1")
+        ki = keep.tile([P, NR], I32, name="ki")
+        ang = keep.tile([P, NR], F32, name="ang")
+        red = keep.tile([P, NR], F32, name="red")
+        ab = keep.tile([P, NR], F32, name="ab")
+        nc.vector.tensor_scalar(out=cst[:, 0:1], in0=pw[:, 0:1], scalar1=1.0 / TWO_PI, scalar2=None, op0=ALU.mult)
+        nc.vector.tensor_scalar(out=ang[:], in0=tokr[:], scalar1=pw[:, 0:1], scalar2=None, op0=ALU.mult)
+        nc.vector.tensor_scalar(out=t1[:], in0=tokr[:], scalar1=cst[:, 0:1], scalar2=MAGIC, op0=ALU.mult, op1=ALU.add)
+        nc.vector.tensor_scalar(out=ki[:], in0=t1[:], scalar1=-MAGIC, scalar2=None, op0=ALU.add)
+        nc.vector.scalar_tensor_tensor(out=red[:], in0=ki[:], scalar=-TWO_PI, in1=ang[:], op0=ALU.mult, op1=ALU.add)
+        nc.scalar.activation(out=trig[:, 1, :], in_=red[:], func=ACT.Sin, scale=cst[:, 1:2])
+        nc.scalar.activation(out=ab[:], in_=red[:], func=ACT.Abs)
+        nc.scalar.activation(out=trig[:, 0, :], in_=ab[:], func=ACT.Sin, scale=-1.0, bias=0.5 * math.pi)
+
+        def scale_block():
+            nc.vector.reciprocal(out=sblk[:, 0:1], in_=pb[:, 1:2])
+            for j in range(7):
+                n = 1 << j
+                nc.vector.tensor_scalar(out=sblk[:, n:2 * n], in0=sblk[:, 0:n], scalar1=pw[:, 1 + j:2 + j], scalar2=None, op0=ALU.mult)
+
+        def ratio_start():
+            nc.vector.reciprocal(out=pinv[:], in_=pw[:])
+            nc.vector.tensor_tensor(out=pinv2[:], in0=pinv[:], in1=pinv[:], op=ALU.mult)
+            nc.vector.tensor_tensor(out=rat[:, 0:1], in0=pb[:, 1:2], in1=pb[:, 1:2], op=ALU.mult)
+
+        idv = ident[:].rearrange("p (m e) -> p m e", e=2)
+        swv = swap[:].rearrange("p (m e) -> p m e", e=2)
+        nc.vector.tensor_copy(out=swv[:, :, 0:1], in_=idv[:, :, 1:2])
+        nc.vector.tensor_copy(out=swv[:, :, 1:2], in_=idv[:, :, 0:1])
+
+        def step_factors():
+            nc.vector.tensor_tensor(out=dco[:], in0=trig[:, :, P:NR], in1=pw[:, 8:NE].unsqueeze(1).to_broadcast([P, 2, 3]),
+                                    op=ALU.mult)
+            nc.vector.tensor_scalar(out=dne[:], in0=dco[:, 1, :], scalar1=-1.0, scalar2=None, op0=ALU.mult)
+
+        def base_block():
+            nc.vector.tensor_tensor(out=cs[0][:, :, 0:P], in0=trig[:, :, 0:P],
+                                    in1=sblk[:].unsqueeze(1).to_broadcast([P, 2, P]), op=ALU.mult)
+
+        tmpd = {}
+
+        def double_s(j):
+            n = P << j
+            tmpd[j] = dp.tile([P, 2, n], F32, tag="tmpd", name="tmpd")
+            nc.scalar.activation(out=tmpd[j][:], in_=cs[0][:, :, 0:n], func=ACT.Copy, scale=dco[:, 0, j:j + 1])
+
+        def double_v(j):
+            n = P << j
+            nc.vector.scalar_tensor_tensor(out=cs[0][:, 0, n:2 * n], in0=cs[0][:, 1, 0:n], scalar=dne[:, j:j + 1],
+                                           in1=tmpd[j][:, 0, :], op0=ALU.mult, op1=ALU.add)
+            nc.vector.scalar_tensor_tensor(out=cs[0][:, 1, n:2 * n], in0=cs[0][:, 0, 0:n], scalar=dco[:, 1, j:j + 1],
+                                           in1=tmpd[j][:, 1, :], op0=ALU.mult, op1=ALU.add)
+
+        def ratio(j):
+            n = 1 << j
+            nc.scalar.activation(out=rat[:, n:2 * n], in_=rat[:, 0:n], func=ACT.Copy, scale=pinv2[:, 1 + j:2 + j])
+
+        csA = [keep.tile([P, 2, HALF], F32, name="csA%d" % mat) for mat in range(2)]
+        ratA = keep.tile([P, HALF], F32, name="ratA")
+        tps = {}
+
+        def turn_t(key, src):
+            tps[key] = pstp.tile([P, HALF], F32, tag="tp", name="tps")
+            for tl in range(4):
+                blk = slice(tl * P, (tl + 1) * P)
+                nc.tensor.transpose(tps[key][:, blk], src[:, blk], ident[:])
+
+        def turn_s(key, dst):
+            nc.scalar.copy(out=dst, in_=tps[key][:])
 
         def twice(ap):
             return ap.unsqueeze(1).to_broadcast([P, 2, HALF])
-        red = {}
 
-        def scales(hf):
-            if PATH[hf] == "B":
-                nc.scalar.activation(out=scl[0][hf][:], in_=tok_b[hf][:], func=ACT.Exp, scale=cl[:, 1:2], bias=cl[:, 2:3])
-                nc.scalar.activation(out=scl[1][hf][:], in_=tok_b[hf][:], func=ACT.Exp, scale=cl[:, 3:4], bias=cl[:, 0:1])
+        def key_tables(hf):
+            if hf == 0:
+                nc.gpsimd.tensor_tensor(out=cs[1][:, :, 0:HALF], in0=cs[0][:, :, 0:HALF], in1=twice(rat[:, 0:HALF]), op=ALU.mult)
             else:
-                arg = keep.tile([P, HALF], F32, name="arg%d" % hf)
-                for tl in range(4):
-                    t = 4 * hf + tl
-                    nc.vector.tensor_scalar(out=arg[:, tl * P:(tl + 1) * P], in0=kl[:], scalar1=pw_a[:, t:t + 1], scalar2=None,
-                                            op0=ALU.mult)
-                nc.scalar.activation(out=scl[0][hf][:], in_=arg[:], func=ACT.Exp)
-                nc.scalar.activation(out=scl[1][hf][:], in_=arg[:], func=ACT.Exp, scale=-1.0)
-
-        def angles_v(hf):
-            t1 = keep.tile([P, HALF], F32, name="t1_%d" % hf)
-            ki = keep.tile([P, HALF], I32, name="ki_%d" % hf)
-            a = keep.tile([P, HALF], F32, name="a_%d" % hf)
-            red[hf] = keep.tile([P, HALF], F32, name="red%d" % hf)
-            if PATH[hf] == "B":
-                nc.vector.tensor_scalar(out=t1[:], in0=tok_b[hf][:], scalar1=cst[:, 2:3], scalar2=MAGIC, op0=ALU.mult, op1=ALU.add)
-                nc.vector.tensor_scalar(out=a[:], in0=tok_b[hf][:], scalar1=cst[:, 0:1], scalar2=None, op0=ALU.mult)
-            else:
-                for tl in range(4):
-                    t = 4 * hf + tl
-                    nc.vector.tensor_scalar(out=a[:, tl * P:(tl + 1) * P], in0=wsgn[:], scalar1=tok_a[:, t:t + 1], scalar2=None,
-                                            op0=ALU.mult)
-                nc.vector.tensor_scalar(out=t1[:], in0=a[:], scalar1=1.0 / TWO_PI, scalar2=MAGIC, op0=ALU.mult, op1=ALU.add)
-            nc.vector.tensor_scalar(out=ki[:], in0=t1[:], scalar1=-MAGIC, scalar2=None, op0=ALU.add)
-            nc.vector.scalar_tensor_tensor(out=red[hf][:], in0=ki[:], scalar=-TWO_PI, in1=a[:], op0=ALU.mult, op1=ALU.add)
-
-        def angles_s(hf):
-            if PATH[hf] == "B":
-                nc.scalar.activation(out=trig[hf][:, 1, :], in_=red[hf][:], func=ACT.Sin, scale=cst[:, 1:2])
-            else:
-                nc.scalar.activation(out=trig[hf][:, 1, :], in_=red[hf][:], func=ACT.Sin)
-            ab = keep.tile([P, HALF], F32, name="ab%d" % hf)
-            nc.scalar.activation(out=ab[:], in_=red[hf][:], func=ACT.Abs)
-            nc.scalar.activation(out=trig[hf][:, 0, :], in_=ab[:], func=ACT.Sin, scale=-1.0, bias=0.5 * math.pi)
-
-        def tables(mat, hf, eng):
-            eng.tensor_tensor(out=cs[mat][hf][:], in0=trig[hf][:], in1=twice(scl[mat][hf][:]), op=ALU.mult)
+                nc.gpsimd.tensor_tensor(out=csA[1][:], in0=csA[0][:], in1=twice(ratA[:]), op=ALU.mult)
 
         xg = [[keep.tile([P, HALF, 4], BF16, name="xg%d_%d" % (g, hf), align_bytes=64) for hf in range(2)] for g in range(2)]
         xc = [[keep.tile([P, HALF], U32, name="xc%d_%d" % (g, hf), align_bytes=64) for hf in range(2)] for g in range(2)]
@@ -252,7 +267,7 @@ def tile_gatedmultiscaleretentionlayer_pa_kernel(tc, x, Wq, bq, Wk, bk, out_0, o
             if eng == "v":
                 nc.vector.tensor_copy(out=dst, in_=src)
             elif eng == "g":
-                nc.gpsimd.tensor_scalar(out=dst, in0=src, scalar1=1.0, scalar2=0.0, op0=ALU.mult, op1=ALU.add)
+                nc.gpsimd.tensor_copy(out=dst, in_=src)
             else:
                 nc.scalar.copy(out=dst, in_=src)
 
@@ -262,16 +277,15 @@ def tile_gatedmultiscaleretentionlayer_pa_kernel(tc, x, Wq, bq, Wk, bk, out_0, o
             ws[a] = wcp.tile([P, 2 * n * DK], U8, tag="ws", name="ws", align_bytes=64)
             nc.vector.quantize_mx(out=wc[a][:].bitcast(FP8X4), scales=ws[a][:], in_=g4[a][:].rearrange("p g c j -> p (g c j)"))
 
-        def mx(i):
+        def mx_half(i, hf):
             a, n = unit_of[i]
-            acc[i] = [psmx.tile([P, HALF], F32, tag="mx", name="acc%d" % hf) for hf in range(2)]
-            for hf in (1, 0):
-                for g in range(2):
-                    c0 = (g * n + i - a) * DK
-                    nc.tensor.matmul_mx(out=acc[i][hf][:],
-                                        lhsT=wc[a][:, c0:c0 + DK].bitcast(FP8X4), lhsT_scale=ws[a][:, c0:c0 + DK],
-                                        rhs=xc[g][hf][:].bitcast(FP8X4), rhs_scale=xs[g][hf][:],
-                                        start=(g == 0), stop=(g == 1))
+            acc[(i, hf)] = psmx.tile([P, HALF], F32, tag="mx", name="acc%d" % hf)
+            for g in range(2):
+                c0 = (g * n + i - a) * DK
+                nc.tensor.matmul_mx(out=acc[(i, hf)][:],
+                                    lhsT=wc[a][:, c0:c0 + DK].bitcast(FP8X4), lhsT_scale=ws[a][:, c0:c0 + DK],
+                                    rhs=xc[g][hf][:].bitcast(FP8X4), rhs_scale=xs[g][hf][:],
+                                    start=(g == 0), stop=(g == 1))
 
         def store(i, hf, osb):
             nc.sync.dma_start(out=outv[i // H][i % H][:, 4 * hf:4 * hf + 4, :], in_=osb[:])
@@ -279,14 +293,14 @@ def tile_gatedmultiscaleretentionlayer_pa_kernel(tc, x, Wq, bq, Wk, bk, out_0, o
         def rot_b(i, hf):
             mat = i // H
             w = bp.tile([P, 2, HALF], F32, tag="uv")
-            nc.vector.scalar_tensor_tensor(out=w[:], in0=twice(acc[i][hf][:]), scalar=biasT[:, i:i + 1], in1=cs[mat][hf][:],
+            nc.vector.scalar_tensor_tensor(out=w[:], in0=twice(acc[(i, hf)][:]), scalar=biasT[:, i:i + 1], in1=cs[mat][:, :, 0:HALF],
                                            op0=ALU.add, op1=ALU.mult)
             uv[(i, hf)] = w
 
         def rot_g(i, hf):
             mat = i // H
             w = gp.tile([P, 2, HALF], F32, tag="uvg")
-            nc.gpsimd.tensor_tensor(out=w[:], in0=twice(tsb[(i, hf)][:]), in1=cs[mat][hf][:], op=ALU.mult)
+            nc.gpsimd.tensor_tensor(out=w[:], in0=twice(tsb[(i, hf)][:]), in1=cs[mat][:, :, 0:HALF], op=ALU.mult)
             uv[(i, hf)] = w
 
         def back_b(i, hf):
@@ -305,7 +319,7 @@ def tile_gatedmultiscaleretentionlayer_pa_kernel(tc, x, Wq, bq, Wk, bk, out_0, o
 
         def evac_a(i, hf):
             tsb[(i, hf)] = ap.tile([P, HALF], F32, tag="t", name="tsb")
-            nc.scalar.activation(out=tsb[(i, hf)][:], in_=acc[i][hf][:], func=ACT.Identity, bias=biasT[:, i:i + 1])
+            nc.scalar.activation(out=tsb[(i, hf)][:], in_=acc[(i, hf)][:], func=ACT.Identity, bias=biasT[:, i:i + 1])
 
         def back_a(i, hf):
             o = pstp.tile([P, 4, DK], F32, tag="tp")
@@ -317,7 +331,7 @@ def tile_gatedmultiscaleretentionlayer_pa_kernel(tc, x, Wq, bq, Wk, bk, out_0, o
             mat = i // H
             o = otp[(i, hf)]
             w = ap.tile([P, 2, HALF], F32, tag="uva")
-            nc.vector.tensor_tensor(out=w[:], in0=twice(o[:].rearrange("p t f -> p (t f)")), in1=cs[mat][hf][:], op=ALU.mult)
+            nc.vector.tensor_tensor(out=w[:], in0=twice(o[:].rearrange("p t f -> p (t f)")), in1=csA[mat][:], op=ALU.mult)
             uv[(i, hf)] = w
 
         def add_a(i, hf):
@@ -329,69 +343,92 @@ def tile_gatedmultiscaleretentionlayer_pa_kernel(tc, x, Wq, bq, Wk, bk, out_0, o
                               in1=w[:, 1, :].rearrange("p (n e) -> p n e", e=2)[:, :, ::-1], op=ALU.add)
             store(i, hf, osb)
 
-        scales(0)
-        scales(1)
-        angles_v(0)
-        angles_s(0)
-        angles_v(1)
-        x_pair(0, "vv")
+        scale_block()
+        step_factors()
+        base_block()
+        ratio_start()
+        x_pair(0, "ss")
         keep_warm(2)
+        double_s(0)
+        x_pair(1, "ss")
+        keep_warm(2)
+        double_v(0)
         x_quant(0)
-        x_pair(1, "vv")
-        keep_warm(2)
-        x_quant(1)
-        angles_s(1)
+        double_s(1)
+        for j in range(8):
+            ratio(j)
         inter(0, "v")
+        double_v(1)
+        x_quant(1)
         quant(0)
+        inter(1, HEAD_ENG)
         bt_ps = pstp.tile([P, P], BF16, tag="tp")
         nc.tensor.transpose(bt_ps[:], btile[:], ident_bf[:])
-        biasT = keep.tile([P, 2 * H], F32, name="biasT")
-        nc.vector.tensor_copy(out=biasT[:], in_=bt_ps[:, 0:2 * H])
         x_pair(2, "ss")
         keep_warm(2)
+        mx_half(0, 0)
+        biasT = keep.tile([P, 2 * H], F32, name="biasT")
+        nc.vector.tensor_copy(out=biasT[:], in_=bt_ps[:, 0:2 * H])
         x_pair(3, "ss")
-        tables(0, 0, nc.vector)
-        tables(0, 1, nc.vector)
-        inter(1, "s")
+        double_s(2)
+        ratio(8)
+        ratio(9)
         x_quant(2)
+        rot_b(0, 0)
         x_quant(3)
+        mx_half(0, 1)
         quant(1)
-        inter(2, "v")
-        inter(3, "v")
+        double_v(2)
+        inter(2, HEAD_ENG)
+        inter(3, HEAD_ENG)
+        quant(2)
+        inter(4, ENG45)
+        inter(5, ENG45)
 
-        def tiles_at(t, kind):
-            if not 0 <= t < NT:
-                return []
-            if kind == "A":
-                return [(t, 1)]
-            if (kind == "G") == g_rot(t):
-                return [(t, 0)]
-            return []
+        NP = NT // 2
 
-        for s in range(NT + 6):
-            if s < NT:
-                mx(s)
-            for b in tiles_at(s - 1, "A") + tiles_at(s - 1, "G"):
-                evac_a(b[0], b[1])
-            for b in tiles_at(s - 1, "B"):
-                rot_b(b[0], b[1])
-            for b in tiles_at(s - 3, "A"):
-                rot_a(b[0], b[1])
-            for b in tiles_at(s - 3, "B") + tiles_at(s - 5, "G"):
-                leave_b(b[0], b[1])
-            for b in tiles_at(s - 4, "A"):
-                add_a(b[0], b[1])
-            for b in tiles_at(s - 2, "G"):
-                rot_g(b[0], b[1])
-            if s % 2 == 0 and s + 2 < NT:
-                quant(s + 2)
-            for b in tiles_at(s - 2, "A"):
-                back_a(b[0], b[1])
-            for b in tiles_at(s - 2, "B") + tiles_at(s - 4, "G"):
-                back_b(b[0], b[1])
-            if s + 4 < NT:
-                inter(s + 4, inter_engine(s + 4))
-            if s % 4 == 2 and 3 <= (s + 10) // 4 < 8:
-                load_w((s + 10) // 4, 0, HALF)
-            if s == 4 or s == 6:
-                tables(1, (s - 4) // 2, nc.gpsimd)
+        def is_g(i):
+            return i % GM == 1 and 4 <= i < 30
+
+        for p in range(NP + 2):
+            heads = (2 * p, 2 * p + 1) if p < NP else ()
+            before = (2 * p - 2, 2 * p - 1) if 1 <= p <= NP else ()
+            for i in heads:
+                if i > 0:
+                    mx_half(i, 0)
+                    mx_half(i, 1)
+            if p == 0:
+                turn_t("c", cs[0][:, 0, HALF:S])
+                turn_t("s", cs[0][:, 1, HALF:S])
+            for i in heads:
+                evac_a(i, 1)
+                if is_g(i):
+                    evac_a(i, 0)
+                    rot_g(i, 0)
+                elif i > 0:
+                    rot_b(i, 0)
+            if p == 0:
+                turn_s("c", csA[0][:, 0, :])
+                turn_s("s", csA[0][:, 1, :])
+            for i in before:
+                back_a(i, 1)
+            for i in before:
+                back_b(i, 0)
+            for i in before:
+                rot_a(i, 1)
+            if 2 * p + 4 < NT:
+                quant(2 * p + 4)
+            for i in (2 * p + 6, 2 * p + 7):
+                if i < NT:
+                    inter(i, inter_engine(i))
+            for i in before:
+                leave_b(i, 0)
+            for i in before:
+                add_a(i, 1)
+            if p < 5:
+                load_w(p + 3, 0, HALF)
+            if p == 0:
+                turn_t("r", rat[:, HALF:S])
+                turn_s("r", ratA[:])
+                key_tables(0)
+                key_tables(1)

@@ -28,7 +28,7 @@ NT = 2 * H
 INTER_G = ()
 GM = 4
 HEAD_ENG = "v"
-ENG45 = "v"
+ENG45 = "s"
 
 
 def g_rot(i):
@@ -44,7 +44,7 @@ def tile_gatedmultiscaleretentionlayer_pa_kernel(tc, x, Wq, bq, Wk, bk, out_0, o
     with ExitStack() as ctx:
         ctx.enter_context(tc.manual_schedule())
         keep = ctx.enter_context(tc.tile_pool(name="keep", bufs=1))
-        wrp = ctx.enter_context(tc.tile_pool(name="wrp", bufs=8))
+        wrp = ctx.enter_context(tc.tile_pool(name="wrp", bufs=5))
         grp = ctx.enter_context(tc.tile_pool(name="grp", bufs=4))
         wcp = ctx.enter_context(tc.tile_pool(name="wcp", bufs=4))
         bp = ctx.enter_context(tc.tile_pool(name="bp", bufs=3))
@@ -393,6 +393,8 @@ def tile_gatedmultiscaleretentionlayer_pa_kernel(tc, x, Wq, bq, Wk, bk, out_0, o
         for p in range(NP + 2):
             heads = (2 * p, 2 * p + 1) if p < NP else ()
             before = (2 * p - 2, 2 * p - 1) if 1 <= p <= NP else ()
+            if p % 2 == 1 and (p + 5) // 2 < 8:
+                load_w((p + 5) // 2, 0, HALF)
             for i in heads:
                 if i > 0:
                     mx_half(i, 0)
@@ -425,8 +427,6 @@ def tile_gatedmultiscaleretentionlayer_pa_kernel(tc, x, Wq, bq, Wk, bk, out_0, o
                 leave_b(i, 0)
             for i in before:
                 add_a(i, 1)
-            if p < 5:
-                load_w(p + 3, 0, HALF)
             if p == 0:
                 turn_t("r", rat[:, HALF:S])
                 turn_s("r", ratA[:])

@@ -32,7 +32,7 @@ ENG45 = "s"
 
 
 def g_rot(i):
-    return i % GM == 1 and i < 30
+    return i % GM == 1 and 4 <= i < 28
 
 
 def inter_engine(i):
@@ -115,9 +115,9 @@ def tile_gatedmultiscaleretentionlayer_pa_kernel(tc, x, Wq, bq, Wk, bk, out_0, o
         pw = keep.tile([P, NE], F32, name="pw")
         nc.vector.memset(pb[:, 0:1], 10000.0)
         nc.vector.tensor_scalar(out=pe[:, 0:1], in0=col[:, 0:1], scalar1=-1.0 / DK, scalar2=None, op0=ALU.mult)
-        nc.gpsimd.tensor_tensor(out=pw[:, 0:1], in0=pb[:, 0:1], in1=pe[:, 0:1], op=ALU.pow)
         nc.vector.tensor_scalar(out=pb[:, 1:NE], in0=col[:, 0:1].to_broadcast([P, NE - 1]), scalar1=1.0 / (1.4 * DK),
                                 scalar2=0.4 / 1.4, op0=ALU.mult, op1=ALU.add)
+        nc.gpsimd.tensor_tensor(out=pw[:, 0:1], in0=pb[:, 0:1], in1=pe[:, 0:1], op=ALU.pow)
         for j in range(7):
             nc.vector.memset(pe[:, 1 + j:2 + j], float(1 << j) / 64.0)
         for j in range(3):
@@ -385,50 +385,50 @@ def tile_gatedmultiscaleretentionlayer_pa_kernel(tc, x, Wq, bq, Wk, bk, out_0, o
         inter(4, ENG45)
         inter(5, ENG45)
 
-        NP = NT // 2
+        def tiles_at(t, kind):
+            if not 0 <= t < NT:
+                return []
+            if kind == "A":
+                return [(t, 1)]
+            if (kind == "G") == g_rot(t):
+                return [(t, 0)]
+            return []
 
-        def is_g(i):
-            return i % GM == 1 and 4 <= i < 30
-
-        for p in range(NP + 2):
-            heads = (2 * p, 2 * p + 1) if p < NP else ()
-            before = (2 * p - 2, 2 * p - 1) if 1 <= p <= NP else ()
-            if p % 2 == 1 and (p + 5) // 2 < 8:
-                load_w((p + 5) // 2, 0, HALF)
-            for i in heads:
-                if i > 0:
-                    mx_half(i, 0)
-                    mx_half(i, 1)
-            if p == 0:
+        for s in range(NT + 6):
+            if 1 <= s < NT:
+                mx_half(s, 1)
+                mx_half(s, 0)
+            if s == 0:
                 turn_t("c", cs[0][:, 0, HALF:S])
                 turn_t("s", cs[0][:, 1, HALF:S])
-            for i in heads:
-                evac_a(i, 1)
-                if is_g(i):
-                    evac_a(i, 0)
-                    rot_g(i, 0)
-                elif i > 0:
-                    rot_b(i, 0)
-            if p == 0:
+            for b in tiles_at(s - 1, "A") + tiles_at(s - 1, "G"):
+                evac_a(b[0], b[1])
+            if s == 1:
                 turn_s("c", csA[0][:, 0, :])
                 turn_s("s", csA[0][:, 1, :])
-            for i in before:
-                back_a(i, 1)
-            for i in before:
-                back_b(i, 0)
-            for i in before:
-                rot_a(i, 1)
-            if 2 * p + 4 < NT:
-                quant(2 * p + 4)
-            for i in (2 * p + 6, 2 * p + 7):
-                if i < NT:
-                    inter(i, inter_engine(i))
-            for i in before:
-                leave_b(i, 0)
-            for i in before:
-                add_a(i, 1)
-            if p == 0:
                 turn_t("r", rat[:, HALF:S])
+            for b in tiles_at(s - 1, "B"):
+                if b[0] > 0:
+                    rot_b(b[0], b[1])
+            for b in tiles_at(s - 3, "A"):
+                rot_a(b[0], b[1])
+            for b in tiles_at(s - 3, "B") + tiles_at(s - 5, "G"):
+                leave_b(b[0], b[1])
+            for b in tiles_at(s - 4, "A"):
+                add_a(b[0], b[1])
+            for b in tiles_at(s - 2, "G"):
+                rot_g(b[0], b[1])
+            if s % 2 == 0 and 4 <= s + 2 < NT:
+                quant(s + 2)
+            for b in tiles_at(s - 2, "A"):
+                back_a(b[0], b[1])
+            for b in tiles_at(s - 2, "B") + tiles_at(s - 4, "G"):
+                back_b(b[0], b[1])
+            if 6 <= s + 4 < NT:
+                inter(s + 4, "s")
+            if s % 4 == 2 and 3 <= (s + 10) // 4 < 8:
+                load_w((s + 10) // 4, 0, HALF)
+            if s == 2:
                 turn_s("r", ratA[:])
                 key_tables(0)
                 key_tables(1)

@@ -27,6 +27,7 @@ MAGIC = 12582912.0
 NT = 2 * H
 INTER_G = ()
 GM = 4
+IL = 6
 HEAD_ENG = "v"
 ENG45 = "s"
 
@@ -45,8 +46,8 @@ def tile_gatedmultiscaleretentionlayer_pa_kernel(tc, x, Wq, bq, Wk, bk, out_0, o
         ctx.enter_context(tc.manual_schedule())
         keep = ctx.enter_context(tc.tile_pool(name="keep", bufs=1))
         wrp = ctx.enter_context(tc.tile_pool(name="wrp", bufs=5))
-        grp = ctx.enter_context(tc.tile_pool(name="grp", bufs=4))
-        wcp = ctx.enter_context(tc.tile_pool(name="wcp", bufs=4))
+        grp = ctx.enter_context(tc.tile_pool(name="grp", bufs=3))
+        wcp = ctx.enter_context(tc.tile_pool(name="wcp", bufs=3))
         bp = ctx.enter_context(tc.tile_pool(name="bp", bufs=3))
         gp = ctx.enter_context(tc.tile_pool(name="gp", bufs=2))
         dp = ctx.enter_context(tc.tile_pool(name="dp", bufs=2))
@@ -245,10 +246,9 @@ def tile_gatedmultiscaleretentionlayer_pa_kernel(tc, x, Wq, bq, Wk, bk, out_0, o
                 nc.vector.quantize_mx(out=xc[g][hf][:, c0:c0 + 256].bitcast(FP8X4), scales=xs[g][hf][:, c0:c0 + 256],
                                       in_=xg[g][hf][:, c0:c0 + 256, :].rearrange("p c j -> p (c j)"))
 
-        unit_of = {0: (0, 1), 1: (1, 1)}
-        for a0 in range(2, NT, 2):
-            unit_of[a0] = (a0, 2)
-            unit_of[a0 + 1] = (a0, 2)
+        unit_of = {0: (0, 1), 1: (1, 1), 2: (2, 2), 3: (2, 2)}
+        for i in range(4, NT):
+            unit_of[i] = (i // 4 * 4, 4)
         g4 = {}
         wc = {}
         ws = {}
@@ -318,7 +318,7 @@ def tile_gatedmultiscaleretentionlayer_pa_kernel(tc, x, Wq, bq, Wk, bk, out_0, o
             store(i, hf, osb)
 
         def evac_a(i, hf):
-            tsb[(i, hf)] = ap.tile([P, HALF], F32, tag="t", name="tsb")
+            tsb[(i, hf)] = ap.tile([P, HALF], F32, tag="tg" if hf == 0 and g_rot(i) else "t", name="tsb")
             nc.scalar.activation(out=tsb[(i, hf)][:], in_=acc[(i, hf)][:], func=ACT.Identity, bias=biasT[:, i:i + 1])
 
         def back_a(i, hf):
@@ -418,14 +418,14 @@ def tile_gatedmultiscaleretentionlayer_pa_kernel(tc, x, Wq, bq, Wk, bk, out_0, o
                 add_a(b[0], b[1])
             for b in tiles_at(s - 2, "G"):
                 rot_g(b[0], b[1])
-            if s % 2 == 0 and 4 <= s + 2 < NT:
+            if s % 4 == 2 and s + 2 < NT:
                 quant(s + 2)
             for b in tiles_at(s - 2, "A"):
                 back_a(b[0], b[1])
             for b in tiles_at(s - 2, "B") + tiles_at(s - 4, "G"):
                 back_b(b[0], b[1])
-            if 6 <= s + 4 < NT:
-                inter(s + 4, "s")
+            if 6 <= s + IL < NT:
+                inter(s + IL, "s")
             if s % 4 == 2 and 3 <= (s + 10) // 4 < 8:
                 load_w((s + 10) // 4, 0, HALF)
             if s == 2:

from contextlib import ExitStack
import math

import concourse.mybir as mybir
from concourse.masks import make_identity

FLOPS = 2 * 1024 * 1024 * 4096

F32 = mybir.dt.float32
BF16 = mybir.dt.bfloat16
I32 = mybir.dt.int32
U32 = mybir.dt.uint32
U8 = mybir.dt.uint8
FP8X4 = mybir.dt.float8_e5m2_x4
ALU = mybir.AluOpType
ACT = mybir.ActivationFunctionType

P = 128
S = 1024
D = 1024
H = 16
DK = 128
TB = 8
HALF = 512
TWO_PI = 2.0 * math.pi
MAGIC = 12582912.0
NT = 2 * H
INTER_G = ()
GM = 4
IL = 6
HEAD_ENG = "v"
ENG45 = "s"


def g_rot(i):
    return i % GM == 1 and 4 <= i < 28


def inter_engine(i):
    return "g" if i in INTER_G else "s"


def tile_gatedmultiscaleretentionlayer_pa_kernel(tc, x, Wq, bq, Wk, bk, out_0, out_1):
    nc = tc.nc
    with ExitStack() as ctx:
        ctx.enter_context(tc.manual_schedule())
        keep = ctx.enter_context(tc.tile_pool(name="keep", bufs=1))
        wrp = ctx.enter_context(tc.tile_pool(name="wrp", bufs=5))
        grp = ctx.enter_context(tc.tile_pool(name="grp", bufs=3))
        wcp = ctx.enter_context(tc.tile_pool(name="wcp", bufs=3))
        bp = ctx.enter_context(tc.tile_pool(name="bp", bufs=3))
        gp = ctx.enter_context(tc.tile_pool(name="gp", bufs=2))
        dp = ctx.enter_context(tc.tile_pool(name="dp", bufs=2))
        ap = ctx.enter_context(tc.tile_pool(name="ap", bufs=4))
        outp = ctx.enter_context(tc.tile_pool(name="outp", bufs=8))
        psmx = ctx.enter_context(tc.psum_pool(name="psmx", bufs=4))
        pstp = ctx.enter_context(tc.psum_pool(name="pstp", bufs=4))

        xv = x.rearrange("b (r t) k -> (b r) t k", t=TB)
        wv = [w.rearrange("(g p j) n -> g p j n", g=2, j=4) for w in (Wq, Wk)]
        outv = [o.rearrange("b h (r t) f -> (b h) r t f", t=TB) for o in (out_0, out_1)]

        x_sb = [keep.tile([P, 2, D], BF16, name="x_sb%d" % tp) for tp in range(4)]
        wraw = {}
        zt = keep.tile([P, HALF], BF16, name="zt")
        btile = keep.tile([P, P], BF16, name="btile")
        nc.vector.memset(btile[:], 0.0)
        nc.vector.memset(zt[:], 0.0)

        def keep_warm(n):
            dps = psmx.tile([P, HALF], F32, tag="mx", name="dps")
            for r in range(n):
                nc.tensor.matmul(out=dps[:], lhsT=zt[:, 0:P], rhs=zt[:], start=True, stop=True)

        keep_warm(5)

        def load_x(tp):
            nc.sync.dma_start(out=x_sb[tp][:], in_=xv[:, 2 * tp:2 * tp + 2, :])

        def load_w(q, c0, c1):
            if c0 == 0:
                wraw[q] = wrp.tile([P, 2, 4, HALF], BF16, tag="wraw", name="wraw")
            for g in range(2):
                nc.sync.dma_start(out=wraw[q][:, g, :, c0:c1], in_=wv[q // 4][g, :, :, (q % 4) * HALF + c0:(q % 4) * HALF + c1])

        load_x(0)
        load_x(1)
        load_w(0, 0, 256)
        load_x(2)
        load_x(3)
        load_w(0, 256, HALF)
        load_w(1, 0, HALF)
        load_w(2, 0, HALF)

        nc.scalar.dma_start(out=btile[0:H, :], in_=bq.rearrange("(h c) -> h c", c=DK))
        nc.scalar.dma_start(out=btile[H:2 * H, :], in_=bk.rearrange("(h c) -> h c", c=DK))
        warm = keep.tile([P, 1], F32, name="warm")
        nc.scalar.activation(out=warm[:], in_=zt[:, 0:1], func=ACT.Sin)

        pidx = keep.tile([P, 1], I32, name="pidx")
        nc.gpsimd.iota(pidx[:], pattern=[[0, 1]], base=0, channel_multiplier=1)
        ident = keep.tile([P, P], F32, name="ident")
        make_identity(nc, ident[:])
        NR = P + 3
        tokr = keep.tile([P, NR], F32, name="tokr")
        nc.gpsimd.iota(tokr[:, 0:P], pattern=[[TB, P]], base=0, channel_multiplier=0, allow_small_or_imprecise_dtypes=True)

        col_i = keep.tile([P, 2], I32, name="col_i")
        col = keep.tile([P, 2], F32, name="col")
        nc.vector.tensor_single_scalar(out=col_i[:, 0:1], in_=pidx[:], scalar=-2, op=ALU.bitwise_and)
        nc.vector.tensor_single_scalar(out=col_i[:, 1:2], in_=pidx[:], scalar=1, op=ALU.bitwise_and)
        nc.vector.tensor_copy(out=col[:], in_=col_i[:])
        NE = 11
        pb = keep.tile([P, NE], F32, name="pb")
        pe = keep.tile([P, NE], F32, name="pe")
        pw = keep.tile([P, NE], F32, name="pw")
        nc.vector.memset(pb[:, 0:1], 10000.0)
        nc.vector.tensor_scalar(out=pe[:, 0:1], in0=col[:, 0:1], scalar1=-1.0 / DK, scalar2=None, op0=ALU.mult)
        nc.vector.tensor_scalar(out=pb[:, 1:NE], in0=col[:, 0:1].to_broadcast([P, NE - 1]), scalar1=1.0 / (1.4 * DK),
                                scalar2=0.4 / 1.4, op0=ALU.mult, op1=ALU.add)
        nc.gpsimd.tensor_tensor(out=pw[:, 0:1], in0=pb[:, 0:1], in1=pe[:, 0:1], op=ALU.pow)
        for j in range(7):
            nc.vector.memset(pe[:, 1 + j:2 + j], float(1 << j) / 64.0)
        for j in range(3):
            nc.vector.memset(pe[:, 8 + j:9 + j], float(1 << j) / 512.0)
            nc.vector.memset(tokr[:, P + j:P + j + 1], float(1 << j))
        nc.gpsimd.tensor_tensor(out=pw[:, 1:NE], in0=pb[:, 1:NE], in1=pe[:, 1:NE], op=ALU.pow)
        ident_bf = keep.tile([P, P], BF16, name="ident_bf")
        make_identity(nc, ident_bf[:])
        cst = keep.tile([P, 2], F32, name="cst")
        nc.vector.tensor_scalar(out=cst[:, 1:2], in0=col[:, 1:2], scalar1=-2.0, scalar2=1.0, op0=ALU.mult, op1=ALU.add)
        swap = keep.tile([P, P], F32, name="swap")

        sblk = keep.tile([P, P], F32, name="sblk")
        trig = keep.tile([P, 2, NR], F32, name="trig")
        cs = [keep.tile([P, 2, S - HALF * mat], F32, name="cs%d" % mat) for mat in range(2)]
        rat = keep.tile([P, S], F32, name="rat")
        pinv = keep.tile([P, NE], F32, name="pinv")
        pinv2 = keep.tile([P, NE], F32, name="pinv2")
        dco = keep.tile([P, 2, 3], F32, name="dco")
        dne = keep.tile([P, 3], F32, name="dne")
        t1 = keep.tile([P, NR], F32, name="t1")
        ki = keep.tile([P, NR], I32, name="ki")
        ang = keep.tile([P, NR], F32, name="ang")
        red = keep.tile([P, NR], F32, name="red")
        ab = keep.tile([P, NR], F32, name="ab")
        nc.vector.tensor_scalar(out=cst[:, 0:1], in0=pw[:, 0:1], scalar1=1.0 / TWO_PI, scalar2=None, op0=ALU.mult)
        nc.vector.tensor_scalar(out=ang[:], in0=tokr[:], scalar1=pw[:, 0:1], scalar2=None, op0=ALU.mult)
        nc.vector.tensor_scalar(out=t1[:], in0=tokr[:], scalar1=cst[:, 0:1], scalar2=MAGIC, op0=ALU.mult, op1=ALU.add)
        nc.vector.tensor_scalar(out=ki[:], in0=t1[:], scalar1=-MAGIC, scalar2=None, op0=ALU.add)
        nc.vector.scalar_tensor_tensor(out=red[:], in0=ki[:], scalar=-TWO_PI, in1=ang[:], op0=ALU.mult, op1=ALU.add)
        nc.scalar.activation(out=trig[:, 1, :], in_=red[:], func=ACT.Sin, scale=cst[:, 1:2])
        nc.scalar.activation(out=ab[:], in_=red[:], func=ACT.Abs)
        nc.scalar.activation(out=trig[:, 0, :], in_=ab[:], func=ACT.Sin, scale=-1.0, bias=0.5 * math.pi)

        def scale_block():
            nc.vector.reciprocal(out=sblk[:, 0:1], in_=pb[:, 1:2])
            for j in range(7):
                n = 1 << j
                nc.vector.tensor_scalar(out=sblk[:, n:2 * n], in0=sblk[:, 0:n], scalar1=pw[:, 1 + j:2 + j], scalar2=None, op0=ALU.mult)

        def ratio_start():
            nc.vector.reciprocal(out=pinv[:], in_=pw[:])
            nc.vector.tensor_tensor(out=pinv2[:], in0=pinv[:], in1=pinv[:], op=ALU.mult)
            nc.vector.tensor_tensor(out=rat[:, 0:1], in0=pb[:, 1:2], in1=pb[:, 1:2], op=ALU.mult)

        idv = ident[:].rearrange("p (m e) -> p m e", e=2)
        swv = swap[:].rearrange("p (m e) -> p m e", e=2)
        nc.vector.tensor_copy(out=swv[:, :, 0:1], in_=idv[:, :, 1:2])
        nc.vector.tensor_copy(out=swv[:, :, 1:2], in_=idv[:, :, 0:1])

        def step_factors():
            nc.vector.tensor_tensor(out=dco[:], in0=trig[:, :, P:NR], in1=pw[:, 8:NE].unsqueeze(1).to_broadcast([P, 2, 3]),
                                    op=ALU.mult)
            nc.vector.tensor_scalar(out=dne[:], in0=dco[:, 1, :], scalar1=-1.0, scalar2=None, op0=ALU.mult)

        def base_block():
            nc.vector.tensor_tensor(out=cs[0][:, :, 0:P], in0=trig[:, :, 0:P],
                                    in1=sblk[:].unsqueeze(1).to_broadcast([P, 2, P]), op=ALU.mult)

        tmpd = {}

        def double_s(j):
            n = P << j
            tmpd[j] = dp.tile([P, 2, n], F32, tag="tmpd", name="tmpd")
            nc.scalar.activation(out=tmpd[j][:], in_=cs[0][:, :, 0:n], func=ACT.Copy, scale=dco[:, 0, j:j + 1])

        def double_v(j):
            n = P << j
            nc.vector.scalar_tensor_tensor(out=cs[0][:, 0, n:2 * n], in0=cs[0][:, 1, 0:n], scalar=dne[:, j:j + 1],
                                           in1=tmpd[j][:, 0, :], op0=ALU.mult, op1=ALU.add)
            nc.vector.scalar_tensor_tensor(out=cs[0][:, 1, n:2 * n], in0=cs[0][:, 0, 0:n], scalar=dco[:, 1, j:j + 1],
                                           in1=tmpd[j][:, 1, :], op0=ALU.mult, op1=ALU.add)

        def ratio(j):
            n = 1 << j
            nc.scalar.activation(out=rat[:, n:2 * n], in_=rat[:, 0:n], func=ACT.Copy, scale=pinv2[:, 1 + j:2 + j])

        csA = [keep.tile([P, 2, HALF], F32, name="csA%d" % mat) for mat in range(2)]
        ratA = keep.tile([P, HALF], F32, name="ratA")
        tps = {}

        def turn_t(key, src):
            tps[key] = pstp.tile([P, HALF], F32, tag="tp", name="tps")
            for tl in range(4):
                blk = slice(tl * P, (tl + 1) * P)
                nc.tensor.transpose(tps[key][:, blk], src[:, blk], ident[:])

        def turn_s(key, dst):
            nc.scalar.copy(out=dst, in_=tps[key][:])

        def twice(ap):
            return ap.unsqueeze(1).to_broadcast([P, 2, HALF])

        def key_tables(hf):
            if hf == 0:
                nc.gpsimd.tensor_tensor(out=cs[1][:, :, 0:HALF], in0=cs[0][:, :, 0:HALF], in1=twice(rat[:, 0:HALF]), op=ALU.mult)
            else:
                nc.gpsimd.tensor_tensor(out=csA[1][:], in0=csA[0][:], in1=twice(ratA[:]), op=ALU.mult)

        xg = [[keep.tile([P, HALF, 4], BF16, name="xg%d_%d" % (g, hf), align_bytes=64) for hf in range(2)] for g in range(2)]
        xc = [[keep.tile([P, HALF], U32, name="xc%d_%d" % (g, hf), align_bytes=64) for hf in range(2)] for g in range(2)]
        xs = [[keep.tile([P, HALF], U8, name="xs%d_%d" % (g, hf), align_bytes=64) for hf in range(2)] for g in range(2)]

        def x_pair(tp, engines):
            hf = tp // 2
            c0 = (tp % 2) * 256
            for g in range(2):
                xt = pstp.tile([P, 2, 2, P], F32, tag="tp")
                for t2 in range(2):
                    words = x_sb[tp][:, t2, :].bitcast(F32)
                    for u in range(2):
                        nc.tensor.transpose(xt[:, t2, u, :], words[:, 256 * g + u:256 * (g + 1):2], ident[:])
                dst = xg[g][hf][:, c0:c0 + 256, :].rearrange("p c j -> p (c j)").bitcast(F32)
                dst = dst.rearrange("p (t r u) -> p t r u", t=2, u=2)
                src = xt[:].rearrange("p t u r -> p t r u")
                if engines[g] == "v":
                    nc.vector.tensor_copy(out=dst, in_=src)
                else:
                    nc.scalar.copy(out=dst, in_=src)

        def x_quant(tp):
            hf = tp // 2
            c0 = (tp % 2) * 256
            for g in range(2):
                nc.vector.quantize_mx(out=xc[g][hf][:, c0:c0 + 256].bitcast(FP8X4), scales=xs[g][hf][:, c0:c0 + 256],
                                      in_=xg[g][hf][:, c0:c0 + 256, :].rearrange("p c j -> p (c j)"))

        unit_of = {0: (0, 1), 1: (1, 1), 2: (2, 2), 3: (2, 2)}
        for i in range(4, NT):
            unit_of[i] = (i // 4 * 4, 4)
        g4 = {}
        wc = {}
        ws = {}
        acc = {}
        uv = {}
        tsb = {}
        otp = {}

        def inter(i, eng):
            a, n = unit_of[i]
            if i == a:
                g4[a] = grp.tile([P, 2, n * DK, 4], BF16, tag="grp", name="g4", align_bytes=64)
            c0 = (i % 4) * DK
            src = wraw[i // 4][:, :, :, c0:c0 + DK].rearrange("p g j (c q) -> p g c j q", q=4)
            dst = g4[a][:, :, (i - a) * DK:(i - a + 1) * DK, :].rearrange("p g (c q) j -> p g c j q", q=4)
            if eng == "v":
                nc.vector.tensor_copy(out=dst, in_=src)
            elif eng == "g":
                nc.gpsimd.tensor_copy(out=dst, in_=src)
            else:
                nc.scalar.copy(out=dst, in_=src)

        def quant(a):
            n = unit_of[a][1]
            wc[a] = wcp.tile([P, 2 * n * DK], U32, tag="wc", name="wc", align_bytes=64)
            ws[a] = wcp.tile([P, 2 * n * DK], U8, tag="ws", name="ws", align_bytes=64)
            nc.vector.quantize_mx(out=wc[a][:].bitcast(FP8X4), scales=ws[a][:], in_=g4[a][:].rearrange("p g c j -> p (g c j)"))

        def mx_half(i, hf):
            a, n = unit_of[i]
            acc[(i, hf)] = psmx.tile([P, HALF], F32, tag="mx", name="acc%d" % hf)
            for g in range(2):
                c0 = (g * n + i - a) * DK
                nc.tensor.matmul_mx(out=acc[(i, hf)][:],
                                    lhsT=wc[a][:, c0:c0 + DK].bitcast(FP8X4), lhsT_scale=ws[a][:, c0:c0 + DK],
                                    rhs=xc[g][hf][:].bitcast(FP8X4), rhs_scale=xs[g][hf][:],
                                    start=(g == 0), stop=(g == 1))

        def store(i, hf, osb):
            nc.sync.dma_start(out=outv[i // H][i % H][:, 4 * hf:4 * hf + 4, :], in_=osb[:])

        def rot_b(i, hf):
            mat = i // H
            w = bp.tile([P, 2, HALF], F32, tag="uv")
            nc.vector.scalar_tensor_tensor(out=w[:], in0=twice(acc[(i, hf)][:]), scalar=biasT[:, i:i + 1], in1=cs[mat][:, :, 0:HALF],
                                           op0=ALU.add, op1=ALU.mult)
            uv[(i, hf)] = w

        def rot_g(i, hf):
            mat = i // H
            w = gp.tile([P, 2, HALF], F32, tag="uvg")
            nc.gpsimd.tensor_tensor(out=w[:], in0=twice(tsb[(i, hf)][:]), in1=cs[mat][:, :, 0:HALF], op=ALU.mult)
            uv[(i, hf)] = w

        def back_b(i, hf):
            w = uv[(i, hf)]
            o = pstp.tile([P, 4, DK], F32, tag="tp")
            for tl in range(4):
                blk = slice(tl * P, (tl + 1) * P)
                nc.tensor.matmul(out=o[:, tl, :], lhsT=w[:, 0, blk], rhs=ident[:], is_transpose=True, start=True, stop=False)
                nc.tensor.matmul(out=o[:, tl, :], lhsT=w[:, 1, blk], rhs=swap[:], is_transpose=True, start=False, stop=True)
            otp[(i, hf)] = o

        def leave_b(i, hf):
            osb = outp.tile([P, 4, DK], F32, tag="o")
            nc.scalar.copy(out=osb[:], in_=otp[(i, hf)][:])
            store(i, hf, osb)

        def evac_a(i, hf):
            tsb[(i, hf)] = ap.tile([P, HALF], F32, tag="tg" if hf == 0 and g_rot(i) else "t", name="tsb")
            nc.scalar.activation(out=tsb[(i, hf)][:], in_=acc[(i, hf)][:], func=ACT.Identity, bias=biasT[:, i:i + 1])

        def back_a(i, hf):
            o = pstp.tile([P, 4, DK], F32, tag="tp")
            for tl in range(4):
                nc.tensor.transpose(o[:, tl, :], tsb[(i, hf)][:, tl * P:(tl + 1) * P], ident[:])
            otp[(i, hf)] = o

        def rot_a(i, hf):
            mat = i // H
            o = otp[(i, hf)]
            w = ap.tile([P, 2, HALF], F32, tag="uva")
            nc.vector.tensor_tensor(out=w[:], in0=twice(o[:].rearrange("p t f -> p (t f)")), in1=csA[mat][:], op=ALU.mult)
            uv[(i, hf)] = w

        def add_a(i, hf):
            w = uv[(i, hf)]
            osb = outp.tile([P, 4, DK], F32, tag="o")
            eng = nc.vector if i >= 31 else nc.gpsimd
            eng.tensor_tensor(out=osb[:].rearrange("p t (m e) -> p (t m) e", e=2),
                              in0=w[:, 0, :].rearrange("p (n e) -> p n e", e=2),
                              in1=w[:, 1, :].rearrange("p (n e) -> p n e", e=2)[:, :, ::-1], op=ALU.add)
            store(i, hf, osb)

        scale_block()
        step_factors()
        base_block()
        ratio_start()
        x_pair(0, "ss")
        keep_warm(2)
        double_s(0)
        x_pair(1, "ss")
        keep_warm(2)
        double_v(0)
        x_quant(0)
        double_s(1)
        for j in range(8):
            ratio(j)
        inter(0, "v")
        double_v(1)
        x_quant(1)
        quant(0)
        inter(1, HEAD_ENG)
        bt_ps = pstp.tile([P, P], BF16, tag="tp")
        nc.tensor.transpose(bt_ps[:], btile[:], ident_bf[:])
        x_pair(2, "ss")
        keep_warm(2)
        mx_half(0, 0)
        biasT = keep.tile([P, 2 * H], F32, name="biasT")
        nc.vector.tensor_copy(out=biasT[:], in_=bt_ps[:, 0:2 * H])
        x_pair(3, "ss")
        double_s(2)
        ratio(8)
        ratio(9)
        x_quant(2)
        rot_b(0, 0)
        x_quant(3)
        mx_half(0, 1)
        quant(1)
        double_v(2)
        inter(2, HEAD_ENG)
        inter(3, HEAD_ENG)
        quant(2)
        inter(4, ENG45)
        inter(5, ENG45)

        def tiles_at(t, kind):
            if not 0 <= t < NT:
                return []
            if kind == "A":
                return [(t, 1)]
            if (kind == "G") == g_rot(t):
                return [(t, 0)]
            return []

        for s in range(NT + 6):
            if 1 <= s < NT:
                mx_half(s, 1)
                mx_half(s, 0)
            if s == 0:
                turn_t("c", cs[0][:, 0, HALF:S])
                turn_t("s", cs[0][:, 1, HALF:S])
            for b in tiles_at(s - 1, "A") + tiles_at(s - 1, "G"):
                evac_a(b[0], b[1])
            if s == 1:
                turn_s("c", csA[0][:, 0, :])
                turn_s("s", csA[0][:, 1, :])
                turn_t("r", rat[:, HALF:S])
            for b in tiles_at(s - 1, "B"):
                if b[0] > 0:
                    rot_b(b[0], b[1])
            for b in tiles_at(s - 3, "A"):
                rot_a(b[0], b[1])
            for b in tiles_at(s - 3, "B") + tiles_at(s - 5, "G"):
                leave_b(b[0], b[1])
            for b in tiles_at(s - 4, "A"):
                add_a(b[0], b[1])
            for b in tiles_at(s - 2, "G"):
                rot_g(b[0], b[1])
            if s % 4 == 2 and s + 2 < NT:
                quant(s + 2)
            for b in tiles_at(s - 2, "A"):
                back_a(b[0], b[1])
            for b in tiles_at(s - 2, "B") + tiles_at(s - 4, "G"):
                back_b(b[0], b[1])
            if 6 <= s + IL < NT:
                inter(s + IL, "s")
            if s % 4 == 2 and 3 <= (s + 10) // 4 < 8:
                load_w((s + 10) // 4, 0, HALF)
            if s == 2:
                turn_s("r", ratA[:])
                key_tables(0)
                key_tables(1)
